import numpy as np
import ml_dtypes


def mxq(x, axis, fmt="e4m3"):
    dtype, down = {"e4m3": (ml_dtypes.float8_e4m3fn, 7), "e5m2": (ml_dtypes.float8_e5m2, 14)}[fmt]
    v = np.moveaxis(np.asarray(x, np.float32).astype(ml_dtypes.bfloat16).astype(np.float64), axis, -1)
    blocks = v.reshape(v.shape[:-1] + (-1, 32))
    amax = np.abs(blocks).max(-1, keepdims=True)
    byte = np.maximum(np.where(amax > 0, np.frexp(amax)[1] - 1 + 127, 0) - down, 1)
    scale = np.exp2(byte - 127.0)
    codes = (blocks / scale).astype(np.float32).astype(dtype).astype(np.float64)
    return np.moveaxis((codes * scale).reshape(v.shape), -1, axis)


WIDE = False


def mx_kscale(k):
    if not WIDE:
        return np.ones(k)
    levels = np.array([10, -10, 5, -5, 0])
    a = np.random.permutation(np.resize(levels, k // 512 * 4)).reshape(k // 512, 4)
    idx = np.arange(k)
    return np.exp2(a[idx // 512, idx % 128 // 32])


BF16 = ml_dtypes.bfloat16


def bf(x):
    return np.asarray(x, np.float32).astype(BF16)


def f64(x):
    return np.asarray(x).astype(np.float64)


B, L, D, H, P, W = 2, 192, 1024, 4, 64, 128
C = 3 * D
EPS = 1e-5


def sigmoid(v):
    return 1.0 / (1.0 + np.exp(-v))


def layernorm(m, g, b):
    mu = m.mean(-1, keepdims=True)
    var = m.var(-1, keepdims=True)
    return (m - mu) / np.sqrt(var + EPS) * g + b


def setup_inputs():
    s = mx_kscale(C)
    return {"x": bf(np.random.standard_normal((B, L, D))),
            "global_out": bf(np.random.standard_normal((B, L, D)) * s[:D]),
            "local_out": bf(np.random.standard_normal((B, L, D)) * s[D:2 * D]),
            "core_out": bf(np.random.standard_normal((B, L, D)) * 0.5 * s[2 * D:]),
            "gate_w": bf(np.random.standard_normal((C, C)) / np.sqrt(C) / s[:, None]),
            "gate_b": bf(np.random.standard_normal(C) * 0.5),
            "outproj_w": bf(np.random.standard_normal((C, D)) * 2.0 / np.sqrt(C) / s[:, None]),
            "outproj_b": bf(np.random.standard_normal(D) * 0.3),
            "ln_mem_g": bf(1.0 + 0.1 * np.random.standard_normal(D)),
            "ln_mem_b": bf(0.1 * np.random.standard_normal(D))}


def reference(x, global_out, local_out, core_out, gate_w, gate_b, outproj_w, outproj_b, ln_mem_g, ln_mem_b):
    combined = np.concatenate([f64(global_out), f64(local_out), f64(core_out)], axis=-1)
    g = sigmoid((mxq(combined, 2, "e4m3") @ mxq(f64(gate_w), 0, "e4m3")) + f64(gate_b))
    gated = combined * g
    memory_output = (mxq(gated, 2, "e4m3") @ mxq(f64(outproj_w), 0, "e4m3")) + f64(outproj_b)
    return f64(x) + layernorm(memory_output, f64(ln_mem_g), f64(ln_mem_b))

@@ -1,0 +1,353 @@
+from contextlib import ExitStack
+
+import concourse.mybir as mybir
+from concourse.masks import make_identity
+
+BF16 = mybir.dt.bfloat16
+F32 = mybir.dt.float32
+U32 = mybir.dt.uint32
+U8 = mybir.dt.uint8
+FP8X4 = mybir.dt.float8_e4m3fn_x4
+ALU = mybir.AluOpType
+ACT = mybir.ActivationFunctionType
+
+P = 128
+PACK = 4
+K_PASS = P * PACK
+TOKENS = 384
+TOKEN_TILES = TOKENS // P
+D = 1024
+STREAMS = 3
+C = STREAMS * D
+PASSES = C // K_PASS
+PASSES_PER_STREAM = D // K_PASS
+BANK = 512
+HALVES = D // BANK
+EPS = 1e-5
+
+TOKEN_GROUPS = ((0, 256), (256, 128))
+TILES_IN_FIRST_GROUP = 2
+
+BLOCK_COLS = 1024
+WIDE = C // BLOCK_COLS
+CHUNKS = C // P
+CHUNKS_PER_WIDE = BLOCK_COLS // P
+PROJ_EARLY = 2
+VEC_COLS = 512
+RUN = 4
+
+LOOKAHEAD = 4
+Z_BANKS = 2
+BLOCKS_PER_STREAM = PASSES // STREAMS
+
+FLOPS = 2 * TOKENS * C * (C + D)
+
+
+def tile_titanstnt_pb_kernel(
+    tc, x, global_out, local_out, core_out, gate_w, gate_b, outproj_w, outproj_b, ln_mem_g, ln_mem_b, out
+):
+    nc = tc.nc
+    streams = [s.flatten_outer_dims() for s in (global_out, local_out, core_out)]
+    x_rows = x.flatten_outer_dims()
+    out_rows = out.flatten_outer_dims()
+
+    gate_blocks = [("gate", wide, c) for wide in range(WIDE) for c in range(PASSES)]
+    proj_blocks = [("proj", None, g) for g in range(PASSES)]
+    blocks = gate_blocks[:-PASSES] + proj_blocks[:PROJ_EARLY] + gate_blocks[-PASSES:] + proj_blocks[PROJ_EARLY:]
+    n_blocks = len(blocks)
+
+    with ExitStack() as ctx:
+        ctx.enter_context(tc.manual_schedule())
+        keep = ctx.enter_context(tc.tile_pool(name="keep", bufs=1))
+        gate_pool = ctx.enter_context(tc.tile_pool(name="gate_pool", bufs=2))
+        gating = ctx.enter_context(tc.tile_pool(name="gating", bufs=2))
+        acc_pool = ctx.enter_context(tc.psum_pool(name="acc_pool", bufs=1))
+        work = ctx.enter_context(tc.psum_pool(name="work", bufs=2))
+
+        ident = keep.tile([P, P], BF16, name="ident")
+        gate_bias = keep.tile([P, CHUNKS], F32, name="gate_bias")
+        eps = keep.tile([P, 1], F32, name="eps")
+        table_in = keep.tile([P, 1], F32, name="table_in")
+        table_out = keep.tile([P, 1], F32, name="table_out")
+        act_grouped = [
+            keep.tile([P, PASSES, count, PACK], BF16, name="act_grouped%d" % grp, align_bytes=64)
+            for grp, (first, count) in enumerate(TOKEN_GROUPS)
+        ]
+        act_codes = [
+            keep.tile([P, PASSES, count], U32, name="act_codes%d" % grp, align_bytes=64)
+            for grp, (first, count) in enumerate(TOKEN_GROUPS)
+        ]
+        act_scales = [
+            keep.tile([P, PASSES, count], U8, name="act_scales%d" % grp, align_bytes=64)
+            for grp, (first, count) in enumerate(TOKEN_GROUPS)
+        ]
+        gated_codes = [
+            keep.tile([P, PASSES, count], U32, name="gated_codes%d" % grp, align_bytes=64)
+            for grp, (first, count) in enumerate(TOKEN_GROUPS)
+        ]
+        gated_scales = [
+            keep.tile([P, PASSES, count], U8, name="gated_scales%d" % grp, align_bytes=64)
+            for grp, (first, count) in enumerate(TOKEN_GROUPS)
+        ]
+        proj_codes = keep.tile([P, PASSES, D], U32, name="proj_codes", align_bytes=64)
+        proj_scales = keep.tile([P, PASSES, D], U8, name="proj_scales", align_bytes=64)
+        x_sb = keep.tile([P, TOKEN_TILES, D], BF16, name="x_sb")
+        ln_bias = keep.tile([P, D], BF16, name="ln_bias")
+        acc = [
+            [acc_pool.tile([P, BANK], F32, name="acc%d%d" % (a, h)) for h in range(HALVES)]
+            for a in range(TOKEN_TILES)
+        ]
+
+        raw = {}
+        grouped = {}
+        gate_codes = {}
+        gate_scales = {}
+        z = {}
+        gate = {}
+        chunks = {"entered": 0, "left": 0}
+
+        def block_rows(i):
+            kind, wide, c = blocks[i]
+            k_rows = slice(c * K_PASS, (c + 1) * K_PASS)
+            if kind == "gate":
+                return gate_w[k_rows, wide * BLOCK_COLS : (wide + 1) * BLOCK_COLS]
+            return outproj_w[k_rows, :]
+
+        def load_block(i):
+            raw[i] = raw_pool.tile([P, PACK, BLOCK_COLS], BF16, name="raw", tag="raw")
+            nc.sync.dma_start(out=raw[i][:], in_=block_rows(i).rearrange("(t p) n -> p t n", p=P))
+
+        def regroup(copy, dst, src):
+            copy(
+                out=dst.rearrange("p (c i) t -> p c t i", i=RUN),
+                in_=src.rearrange("p t (c i) -> p c t i", i=RUN),
+            )
+
+        def regroup_block(i):
+            grouped[i] = grouped_pool.tile(
+                [P, BLOCK_COLS, PACK], BF16, name="grouped", tag="grouped", align_bytes=64
+            )
+            regroup(nc.vector.tensor_copy, grouped[i][:, :VEC_COLS, :], raw[i][:, :, :VEC_COLS])
+            regroup(nc.scalar.copy, grouped[i][:, VEC_COLS:, :], raw[i][:, :, VEC_COLS:])
+
+        def quantise_block(i):
+            kind, wide, c = blocks[i]
+            if kind == "gate":
+                if c == 0:
+                    gate_codes[wide] = gate_pool.tile(
+                        [P, PASSES, BLOCK_COLS], U32, name="gate_codes", tag="gate_codes", align_bytes=64
+                    )
+                    gate_scales[wide] = gate_pool.tile(
+                        [P, PASSES, BLOCK_COLS], U8, name="gate_scales", tag="gate_scales", align_bytes=64
+                    )
+                codes, scales = gate_codes[wide][:, c, :], gate_scales[wide][:, c, :]
+            else:
+                codes, scales = proj_codes[:, c, :], proj_scales[:, c, :]
+            nc.vector.quantize_mx(
+                out=codes.bitcast(FP8X4), scales=scales, in_=grouped[i][:].rearrange("p n t -> p (n t)")
+            )
+
+        def gate_matmuls(e):
+            wide, piece = divmod(e, CHUNKS_PER_WIDE)
+            cols = slice(piece * P, (piece + 1) * P)
+            z[e] = work.tile([P, TOKENS], F32, name="z", tag="work")
+            for grp, (first, count) in enumerate(TOKEN_GROUPS):
+                for c in range(PASSES):
+                    nc.tensor.matmul_mx(
+                        out=z[e][:, first : first + count],
+                        lhsT=gate_codes[wide][:, c, cols].bitcast(FP8X4),
+                        lhsT_scale=gate_scales[wide][:, c, cols],
+                        rhs=act_codes[grp][:, c, :].bitcast(FP8X4),
+                        rhs_scale=act_scales[grp][:, c, :],
+                        start=(c == 0),
+                        stop=(c == PASSES - 1),
+                    )
+
+        def gate_sigmoid(e):
+            g, t = divmod(e, PACK)
+            if t == 0:
+                gate[g] = gating.tile([P, PACK, TOKENS], F32, name="gate", tag="gate")
+            nc.scalar.activation(
+                out=gate[g][:, t, :], in_=z[e][:], func=ACT.Sigmoid, bias=gate_bias[:, e : e + 1], scale=1.0
+            )
+
+        def gate_product(g):
+            gated = []
+            for grp, (first, count) in enumerate(TOKEN_GROUPS):
+                gated.append(
+                    gating.tile([P, count, PACK], BF16, name="gated%d" % grp, tag="gated%d" % grp, align_bytes=64)
+                )
+                nc.vector.tensor_tensor(
+                    out=gated[grp][:],
+                    in0=gate[g][:, :, first : first + count].rearrange("p t k -> p k t"),
+                    in1=act_grouped[grp][:, g, :, :],
+                    op=ALU.mult,
+                )
+            for grp in range(len(TOKEN_GROUPS)):
+                nc.vector.quantize_mx(
+                    out=gated_codes[grp][:, g, :].bitcast(FP8X4),
+                    scales=gated_scales[grp][:, g, :],
+                    in_=gated[grp][:].rearrange("p k t -> p (k t)"),
+                )
+
+        def project(g):
+            for a in range(TOKEN_TILES):
+                grp, tile_in_group = divmod(a, TILES_IN_FIRST_GROUP)
+                toks = slice(tile_in_group * P, (tile_in_group + 1) * P)
+                for h in range(HALVES):
+                    cols = slice(h * BANK, (h + 1) * BANK)
+                    nc.tensor.matmul_mx(
+                        out=acc[a][h][:],
+                        lhsT=gated_codes[grp][:, g, toks].bitcast(FP8X4),
+                        lhsT_scale=gated_scales[grp][:, g, toks],
+                        rhs=proj_codes[:, g, cols].bitcast(FP8X4),
+                        rhs_scale=proj_scales[:, g, cols],
+                        start=(g == 0),
+                        stop=(g == PASSES - 1),
+                    )
+
+        def step(i):
+            if i < PASSES:
+                advance = 0
+            elif i < n_blocks and blocks[i][0] == "gate":
+                advance = 1
+            else:
+                advance = 2
+            first_left = chunks["left"]
+            chunks["left"] = max(first_left, chunks["entered"] + advance - Z_BANKS)
+            advance = min(advance, CHUNKS - chunks["entered"])
+            for e in range(first_left, chunks["left"]):
+                gate_sigmoid(e)
+            if i < n_blocks:
+                regroup_block(i)
+            if i + LOOKAHEAD < n_blocks:
+                load_block(i + LOOKAHEAD)
+            if i >= 1:
+                quantise_block(i - 1)
+            for e in range(first_left, chunks["left"]):
+                if e % PACK == PACK - 1:
+                    gate_product(e // PACK)
+            for e in range(chunks["entered"], chunks["entered"] + advance):
+                gate_matmuls(e)
+            chunks["entered"] += advance
+            if i >= 1 and blocks[i - 1][0] == "proj":
+                project(blocks[i - 1][2])
+
+        with ExitStack() as stage:
+            raw_pool = stage.enter_context(tc.tile_pool(name="raw_pool", bufs=LOOKAHEAD))
+            grouped_pool = stage.enter_context(tc.tile_pool(name="grouped_pool", bufs=3))
+            acts = stage.enter_context(tc.tile_pool(name="acts", bufs=1))
+
+            act_rows = {}
+            for s in range(STREAMS):
+                for a in range(TOKEN_TILES):
+                    act_rows[s, a] = acts.tile([P, D], BF16, name="act_rows%d%d" % (s, a))
+                    nc.sync.dma_start(out=act_rows[s, a][:], in_=streams[s][a * P : (a + 1) * P, :])
+                for i in range(s * BLOCKS_PER_STREAM, min((s + 1) * BLOCKS_PER_STREAM, LOOKAHEAD)):
+                    load_block(i)
+
+            make_identity(nc, ident[:])
+            bias_rows = acts.tile([P, P], BF16, name="bias_rows")
+            nc.vector.memset(bias_rows[:], 0.0)
+            nc.scalar.dma_start(out=bias_rows[:CHUNKS, :], in_=gate_b.rearrange("(e p) -> e p", p=P))
+            nc.vector.memset(eps[:], EPS)
+            nc.vector.memset(table_in[:], 0.0)
+            nc.scalar.activation(out=table_out[:], in_=table_in[:], func=ACT.Sigmoid)
+            bias_cols = work.tile([P, P], BF16, name="bias_cols", tag="work")
+            nc.tensor.transpose(bias_cols[:], bias_rows[:], ident[:])
+            nc.vector.tensor_copy(out=gate_bias[:], in_=bias_cols[:, :CHUNKS])
+
+            def quantise_stream(s):
+                passes = slice(s * PASSES_PER_STREAM, (s + 1) * PASSES_PER_STREAM)
+                for grp in range(len(TOKEN_GROUPS)):
+                    nc.vector.quantize_mx(
+                        out=act_codes[grp][:, passes, :].rearrange("p c k -> p (c k)").bitcast(FP8X4),
+                        scales=act_scales[grp][:, passes, :].rearrange("p c k -> p (c k)"),
+                        in_=act_grouped[grp][:, passes, :, :].rearrange("p c k t -> p (c k t)"),
+                    )
+
+            for s in range(STREAMS):
+                passes = slice(s * PASSES_PER_STREAM, (s + 1) * PASSES_PER_STREAM)
+                for a in range(TOKEN_TILES):
+                    turned = work.tile([P, D // P, P], BF16, name="turned", tag="work")
+                    for j in range(D // P):
+                        nc.tensor.transpose(turned[:, j, :], act_rows[s, a][:, j * P : (j + 1) * P], ident[:])
+                    grp, tile_in_group = divmod(a, TILES_IN_FIRST_GROUP)
+                    toks = slice(tile_in_group * P, (tile_in_group + 1) * P)
+                    copy = nc.vector.tensor_copy if (s * TOKEN_TILES + a) % 2 == 0 else nc.scalar.copy
+                    copy(
+                        out=act_grouped[grp][:, passes, toks, :],
+                        in_=turned[:].rearrange("p (c t) k -> p c k t", t=PACK),
+                    )
+                    if a < BLOCKS_PER_STREAM:
+                        step(s * BLOCKS_PER_STREAM + a)
+                if s > 0:
+                    quantise_stream(s - 1)
+            quantise_stream(STREAMS - 1)
+
+            for i in range(PASSES, n_blocks + 1):
+                step(i)
+                if i + LOOKAHEAD == n_blocks:
+                    nc.sync.dma_start(out=x_sb[:], in_=x_rows.rearrange("(a p) d -> p a d", p=P))
+                    nc.sync.dma_start(out=ln_bias[:], in_=ln_mem_b.partition_broadcast(P))
+
+        tail = ctx.enter_context(tc.tile_pool(name="tail", bufs=1))
+        proj_bias = tail.tile([P, D], BF16, name="proj_bias")
+        ln_gain = tail.tile([P, D], BF16, name="ln_gain")
+        nc.sync.dma_start(out=proj_bias[:], in_=outproj_b.partition_broadcast(P))
+        nc.sync.dma_start(out=ln_gain[:], in_=ln_mem_g.partition_broadcast(P))
+
+        residual = tail.tile([P, TOKEN_TILES, D], F32, name="residual")
+        nc.vector.tensor_tensor(
+            out=residual[:],
+            in0=x_sb[:],
+            in1=ln_bias[:].unsqueeze(1).to_broadcast([P, TOKEN_TILES, D]),
+            op=ALU.add,
+        )
+
+        nc.scalar.activation(out=table_out[:], in_=eps[:], func=ACT.Sqrt)
+
+        m = {}
+        neg_mean = {}
+        std = {}
+        squares = tail.tile([P, D], BF16, name="squares")
+        for a in range(TOKEN_TILES):
+            m[a] = tail.tile([P, D], F32, name="m%d" % a)
+            sums = tail.tile([P, HALVES], F32, name="sums%d" % a)
+            for h in range(HALVES):
+                cols = slice(h * BANK, (h + 1) * BANK)
+                nc.vector.scalar_tensor_tensor(
+                    out=m[a][:, cols],
+                    in0=acc[a][h][:],
+                    scalar=1.0,
+                    in1=proj_bias[:, cols],
+                    op0=ALU.mult,
+                    op1=ALU.add,
+                    accum_out=sums[:, h : h + 1],
+                )
+            neg_mean[a] = tail.tile([P, 1], F32, name="neg_mean%d" % a)
+            nc.vector.tensor_scalar(
+                out=neg_mean[a][:],
+                in0=sums[:, 0:1],
+                scalar1=sums[:, 1:2],
+                scalar2=-1.0 / D,
+                op0=ALU.add,
+                op1=ALU.mult,
+            )
+            sum_sq = tail.tile([P, 1], F32, name="sum_sq%d" % a)
+            nc.scalar.activation(
+                out=squares[:], in_=m[a][:], func=ACT.Square, bias=neg_mean[a][:], scale=1.0, accum_out=sum_sq[:]
+            )
+            std[a] = tail.tile([P, 1], F32, name="std%d" % a)
+            nc.scalar.activation(out=std[a][:], in_=sum_sq[:], func=ACT.Sqrt, bias=eps[:], scale=1.0 / D)
+
+        for a in range(TOKEN_TILES):
+            nc.vector.scalar_tensor_tensor(
+                out=m[a][:], in0=m[a][:], scalar=neg_mean[a][:], in1=ln_gain[:], op0=ALU.add, op1=ALU.mult
+            )
+            rstd = tail.tile([P, 1], F32, name="rstd%d" % a)
+            nc.vector.reciprocal(out=rstd[:], in_=std[a][:])
+            nc.vector.scalar_tensor_tensor(
+                out=m[a][:], in0=m[a][:], scalar=rstd[:], in1=residual[:, a, :], op0=ALU.mult, op1=ALU.add
+            )
+            nc.sync.dma_start(out=out_rows[a * P : (a + 1) * P, :], in_=m[a][:])

@@ -92,9 +92,11 @@ def tile_titanstnt_pb_kernel(
         proj_codes = keep.tile([P, PASSES, D], U32, name="proj_codes", align_bytes=64)
         proj_scales = keep.tile([P, PASSES, D], U8, name="proj_scales", align_bytes=64)
         x_sb = keep.tile([P, TOKEN_TILES, D], BF16, name="x_sb")
-        ln_bias = keep.tile([P, D], BF16, name="ln_bias")
+        proj_bias = keep.tile([P, D], BF16, name="proj_bias")
+        ones = keep.tile([P, P], BF16, name="ones")
+        ln_bias_row = keep.tile([P, D], BF16, name="ln_bias_row")
         acc = [
-            [acc_pool.tile([P, BANK], F32, name="acc%d%d" % (a, h)) for h in range(HALVES)]
+            [acc_pool.tile([P, BANK], F32, name="acc%d%d" % (a, h), tag="bank%d%d" % (a, h)) for h in range(HALVES)]
             for a in range(TOKEN_TILES)
         ]
 
@@ -253,9 +255,8 @@ def tile_titanstnt_pb_kernel(
             nc.vector.memset(eps[:], EPS)
             nc.vector.memset(table_in[:], 0.0)
             nc.scalar.activation(out=table_out[:], in_=table_in[:], func=ACT.Sigmoid)
-            bias_cols = work.tile([P, P], BF16, name="bias_cols", tag="work")
-            nc.tensor.transpose(bias_cols[:], bias_rows[:], ident[:])
-            nc.vector.tensor_copy(out=gate_bias[:], in_=bias_cols[:, :CHUNKS])
+            nc.vector.memset(ones[:], 1.0)
+            nc.vector.memset(ln_bias_row[:], 0.0)
 
             def quantise_stream(s):
                 passes = slice(s * PASSES_PER_STREAM, (s + 1) * PASSES_PER_STREAM)
@@ -274,7 +275,7 @@ def tile_titanstnt_pb_kernel(
                         nc.tensor.transpose(turned[:, j, :], act_rows[s, a][:, j * P : (j + 1) * P], ident[:])
                     grp, tile_in_group = divmod(a, TILES_IN_FIRST_GROUP)
                     toks = slice(tile_in_group * P, (tile_in_group + 1) * P)
-                    copy = nc.vector.tensor_copy if (s * TOKEN_TILES + a) % 2 == 0 else nc.scalar.copy
+                    copy = nc.vector.tensor_copy if a == 0 else nc.scalar.copy
                     copy(
                         out=act_grouped[grp][:, passes, toks, :],
                         in_=turned[:].rearrange("p (c t) k -> p c k t", t=PACK),
@@ -284,32 +285,27 @@ def tile_titanstnt_pb_kernel(
                 if s > 0:
                     quantise_stream(s - 1)
             quantise_stream(STREAMS - 1)
+            bias_cols = work.tile([P, P], BF16, name="bias_cols", tag="work")
+            nc.tensor.transpose(bias_cols[:], bias_rows[:], ident[:])
+            nc.vector.tensor_copy(out=gate_bias[:], in_=bias_cols[:, :CHUNKS])
 
             for i in range(PASSES, n_blocks + 1):
                 step(i)
                 if i + LOOKAHEAD == n_blocks:
                     nc.sync.dma_start(out=x_sb[:], in_=x_rows.rearrange("(a p) d -> p a d", p=P))
-                    nc.sync.dma_start(out=ln_bias[:], in_=ln_mem_b.partition_broadcast(P))
+                    nc.sync.dma_start(out=ln_bias_row[:1, :], in_=ln_mem_b.unsqueeze(0))
+                    nc.sync.dma_start(out=proj_bias[:], in_=outproj_b.partition_broadcast(P))
 
         tail = ctx.enter_context(tc.tile_pool(name="tail", bufs=1))
-        proj_bias = tail.tile([P, D], BF16, name="proj_bias")
         ln_gain = tail.tile([P, D], BF16, name="ln_gain")
-        nc.sync.dma_start(out=proj_bias[:], in_=outproj_b.partition_broadcast(P))
         nc.sync.dma_start(out=ln_gain[:], in_=ln_mem_g.partition_broadcast(P))
-
-        residual = tail.tile([P, TOKEN_TILES, D], F32, name="residual")
-        nc.vector.tensor_tensor(
-            out=residual[:],
-            in0=x_sb[:],
-            in1=ln_bias[:].unsqueeze(1).to_broadcast([P, TOKEN_TILES, D]),
-            op=ALU.add,
-        )
 
         nc.scalar.activation(out=table_out[:], in_=eps[:], func=ACT.Sqrt)
 
         m = {}
         neg_mean = {}
         std = {}
+        residual = {}
         squares = tail.tile([P, D], BF16, name="squares")
         for a in range(TOKEN_TILES):
             m[a] = tail.tile([P, D], F32, name="m%d" % a)
@@ -340,6 +336,11 @@ def tile_titanstnt_pb_kernel(
             )
             std[a] = tail.tile([P, 1], F32, name="std%d" % a)
             nc.scalar.activation(out=std[a][:], in_=sum_sq[:], func=ACT.Sqrt, bias=eps[:], scale=1.0 / D)
+            for h in range(HALVES):
+                cols = slice(h * BANK, (h + 1) * BANK)
+                residual[a, h] = acc_pool.tile([P, BANK], F32, name="residual%d%d" % (a, h), tag="bank%d%d" % (a, h))
+                nc.tensor.matmul(out=residual[a, h][:], lhsT=ident[:], rhs=x_sb[:, a, cols], start=True, stop=False)
+                nc.tensor.matmul(out=residual[a, h][:], lhsT=ones[:], rhs=ln_bias_row[:, cols], start=False, stop=True)
 
         for a in range(TOKEN_TILES):
             nc.vector.scalar_tensor_tensor(
@@ -347,7 +348,9 @@ def tile_titanstnt_pb_kernel(
             )
             rstd = tail.tile([P, 1], F32, name="rstd%d" % a)
             nc.vector.reciprocal(out=rstd[:], in_=std[a][:])
-            nc.vector.scalar_tensor_tensor(
-                out=m[a][:], in0=m[a][:], scalar=rstd[:], in1=residual[:, a, :], op0=ALU.mult, op1=ALU.add
-            )
-            nc.sync.dma_start(out=out_rows[a * P : (a + 1) * P, :], in_=m[a][:])
+            for h in range(HALVES):
+                cols = slice(h * BANK, (h + 1) * BANK)
+                nc.vector.scalar_tensor_tensor(
+                    out=m[a][:, cols], in0=m[a][:, cols], scalar=rstd[:], in1=residual[a, h][:], op0=ALU.mult, op1=ALU.add
+                )
+                nc.sync.dma_start(out=out_rows[a * P : (a + 1) * P, cols], in_=m[a][:, cols])

@@ -17,6 +17,13 @@ K_PASS = P * PACK
 TOKENS = 384
 TOKEN_TILES = TOKENS // P
 D = 1024
+WORDS = D // 2
+ACT_VEC = ()
+MAX_ADV = 2
+EAGER = 0
+PACE = lambda i: max(0, (3 * (i - 6)) // 2)
+HEAD_LOADS = (("b",0),("b",1),("s",0),("b",2),("b",3),("s",1))
+HEAD = (("b",0),("b",1),("load",2),("s",0),("b",2),("q",0),("b",3),("s",1),("b",4),("q",1),("b",5),("s",2),("b",6),("q",2))
 STREAMS = 3
 C = STREAMS * D
 PASSES = C // K_PASS
@@ -32,8 +39,10 @@ BLOCK_COLS = 1024
 WIDE = C // BLOCK_COLS
 CHUNKS = C // P
 CHUNKS_PER_WIDE = BLOCK_COLS // P
-PROJ_EARLY = 2
+PROJ_EARLY = 1
 VEC_COLS = 512
+PAIR = 2
+HALVES_OF_PASS = 2
 RUN = 4
 
 LOOKAHEAD = 4
@@ -65,6 +74,7 @@ def tile_titanstnt_pb_kernel(
         work = ctx.enter_context(tc.psum_pool(name="work", bufs=2))
 
         ident = keep.tile([P, P], BF16, name="ident")
+        ident_words = keep.tile([P, P], F32, name="ident_words")
         gate_bias = keep.tile([P, CHUNKS], F32, name="gate_bias")
         eps = keep.tile([P, 1], F32, name="eps")
         table_in = keep.tile([P, 1], F32, name="table_in")
@@ -106,7 +116,7 @@ def tile_titanstnt_pb_kernel(
         gate_scales = {}
         z = {}
         gate = {}
-        chunks = {"entered": 0, "left": 0}
+        chunks = {"entered": 0, "left": 0, "weights": 0, "gated": 0, "projected": 0, "ready": 0}
 
         def block_rows(i):
             kind, wide, c = blocks[i]
@@ -117,7 +127,12 @@ def tile_titanstnt_pb_kernel(
 
         def load_block(i):
             raw[i] = raw_pool.tile([P, PACK, BLOCK_COLS], BF16, name="raw", tag="raw")
-            nc.sync.dma_start(out=raw[i][:], in_=block_rows(i).rearrange("(t p) n -> p t n", p=P))
+            for cols in (slice(0, VEC_COLS), slice(VEC_COLS, BLOCK_COLS)) if i == 0 else (slice(0, BLOCK_COLS),):
+                for u in range(HALVES_OF_PASS):
+                    nc.sync.dma_start(
+                        out=raw[i][:, PAIR * u : PAIR * (u + 1), cols],
+                        in_=block_rows(i)[u * 2 * P : (u + 1) * 2 * P, cols].rearrange("(p e) n -> p e n", e=PAIR),
+                    )
 
         def regroup(copy, dst, src):
             copy(
@@ -125,12 +140,24 @@ def tile_titanstnt_pb_kernel(
                 in_=src.rearrange("p t (c i) -> p c t i", i=RUN),
             )
 
+        def regroup_gate(copy, dst, src, first, last):
+            copy(
+                out=dst[:].rearrange("p (e m) t -> p e m t", e=PAIR)[:, :, first // PAIR : last // PAIR, :].rearrange(
+                    "p e (c i) t -> p e c t i", i=RUN
+                ),
+                in_=src[:, :, first:last].rearrange("p t (c i e) -> p e c t i", i=RUN, e=PAIR),
+            )
+
         def regroup_block(i):
             grouped[i] = grouped_pool.tile(
                 [P, BLOCK_COLS, PACK], BF16, name="grouped", tag="grouped", align_bytes=64
             )
-            regroup(nc.vector.tensor_copy, grouped[i][:, :VEC_COLS, :], raw[i][:, :, :VEC_COLS])
-            regroup(nc.scalar.copy, grouped[i][:, VEC_COLS:, :], raw[i][:, :, VEC_COLS:])
+            if blocks[i][0] == "proj":
+                regroup(nc.vector.tensor_copy, grouped[i][:, :VEC_COLS, :], raw[i][:, :, :VEC_COLS])
+                regroup(nc.scalar.copy, grouped[i][:, VEC_COLS:, :], raw[i][:, :, VEC_COLS:])
+            else:
+                regroup_gate(nc.vector.tensor_copy, grouped[i], raw[i], 0, VEC_COLS)
+                regroup_gate(nc.scalar.copy, grouped[i], raw[i], VEC_COLS, BLOCK_COLS)
 
         def quantise_block(i):
             kind, wide, c = blocks[i]
@@ -151,7 +178,9 @@ def tile_titanstnt_pb_kernel(
 
         def gate_matmuls(e):
             wide, piece = divmod(e, CHUNKS_PER_WIDE)
-            cols = slice(piece * P, (piece + 1) * P)
+            column_run, parity = divmod(piece, PAIR)
+            first_col = parity * (BLOCK_COLS // PAIR) + column_run * P
+            cols = slice(first_col, first_col + P)
             z[e] = work.tile([P, TOKENS], F32, name="z", tag="work")
             for grp, (first, count) in enumerate(TOKEN_GROUPS):
                 for c in range(PASSES):
@@ -209,15 +238,15 @@ def tile_titanstnt_pb_kernel(
                     )
 
         def step(i):
-            if i < PASSES:
-                advance = 0
-            elif i < n_blocks and blocks[i][0] == "gate":
-                advance = 1
-            else:
-                advance = 2
+            if i >= 1 and blocks[i - 1][0] == "gate" and blocks[i - 1][2] == PASSES - 1:
+                chunks["ready"] += CHUNKS_PER_WIDE
+            due = PACE(i)
+            advance = max(0, min(due, chunks["ready"]) - chunks["entered"])
+            advance = min(advance, MAX_ADV)
             first_left = chunks["left"]
-            chunks["left"] = max(first_left, chunks["entered"] + advance - Z_BANKS)
-            advance = min(advance, CHUNKS - chunks["entered"])
+            chunks["left"] = max(first_left, min(chunks["entered"], chunks["entered"] + advance - Z_BANKS + EAGER))
+            if i >= n_blocks:
+                chunks["left"] = chunks["entered"]
             for e in range(first_left, chunks["left"]):
                 gate_sigmoid(e)
             if i < n_blocks:
@@ -229,11 +258,15 @@ def tile_titanstnt_pb_kernel(
             for e in range(first_left, chunks["left"]):
                 if e % PACK == PACK - 1:
                     gate_product(e // PACK)
+                    chunks["gated"] += 1
             for e in range(chunks["entered"], chunks["entered"] + advance):
                 gate_matmuls(e)
             chunks["entered"] += advance
             if i >= 1 and blocks[i - 1][0] == "proj":
-                project(blocks[i - 1][2])
+                chunks["weights"] += 1
+            while chunks["projected"] < min(chunks["weights"], chunks["gated"]):
+                project(chunks["projected"])
+                chunks["projected"] += 1
 
         with ExitStack() as stage:
             raw_pool = stage.enter_context(tc.tile_pool(name="raw_pool", bufs=LOOKAHEAD))
@@ -241,17 +274,20 @@ def tile_titanstnt_pb_kernel(
             acts = stage.enter_context(tc.tile_pool(name="acts", bufs=1))
 
             act_rows = {}
-            for s in range(STREAMS):
+
+            def load_stream(s):
                 for a in range(TOKEN_TILES):
                     act_rows[s, a] = acts.tile([P, D], BF16, name="act_rows%d%d" % (s, a))
                     nc.sync.dma_start(out=act_rows[s, a][:], in_=streams[s][a * P : (a + 1) * P, :])
-                for i in range(s * BLOCKS_PER_STREAM, min((s + 1) * BLOCKS_PER_STREAM, LOOKAHEAD)):
-                    load_block(i)
 
-            make_identity(nc, ident[:])
-            bias_rows = acts.tile([P, P], BF16, name="bias_rows")
+            for what, which in HEAD_LOADS:
+                (load_block if what == "b" else load_stream)(which)
+
+            make_identity(nc, ident_words[:])
+            nc.vector.tensor_copy(out=ident[:], in_=ident_words[:])
+            bias_rows = acts.tile([P, PAIR * P], BF16, name="bias_rows")
             nc.vector.memset(bias_rows[:], 0.0)
-            nc.scalar.dma_start(out=bias_rows[:CHUNKS, :], in_=gate_b.rearrange("(e p) -> e p", p=P))
+            nc.scalar.dma_start(out=bias_rows[: CHUNKS // PAIR, :], in_=gate_b.rearrange("(r p) -> r p", p=PAIR * P))
             nc.vector.memset(eps[:], EPS)
             nc.vector.memset(table_in[:], 0.0)
             nc.scalar.activation(out=table_out[:], in_=table_in[:], func=ACT.Sigmoid)
@@ -267,35 +303,40 @@ def tile_titanstnt_pb_kernel(
                         in_=act_grouped[grp][:, passes, :, :].rearrange("p c k t -> p (c k t)"),
                     )
 
-            for s in range(STREAMS):
+            def do_stream(s):
                 passes = slice(s * PASSES_PER_STREAM, (s + 1) * PASSES_PER_STREAM)
                 for a in range(TOKEN_TILES):
-                    turned = work.tile([P, D // P, P], BF16, name="turned", tag="work")
-                    for j in range(D // P):
-                        nc.tensor.transpose(turned[:, j, :], act_rows[s, a][:, j * P : (j + 1) * P], ident[:])
+                    turned = work.tile([P, WORDS // P, P], F32, name="turned", tag="work")
+                    for j in range(WORDS // P):
+                        nc.tensor.transpose(
+                            turned[:, j, :], act_rows[s, a][:].bitcast(F32)[:, j * P : (j + 1) * P], ident_words[:]
+                        )
                     grp, tile_in_group = divmod(a, TILES_IN_FIRST_GROUP)
                     toks = slice(tile_in_group * P, (tile_in_group + 1) * P)
-                    copy = nc.vector.tensor_copy if a == 0 else nc.scalar.copy
+                    copy = nc.vector.tensor_copy if a in ACT_VEC else nc.scalar.copy
                     copy(
-                        out=act_grouped[grp][:, passes, toks, :],
-                        in_=turned[:].rearrange("p (c t) k -> p c k t", t=PACK),
+                        out=act_grouped[grp][:, passes, toks, :].bitcast(F32),
+                        in_=turned[:].rearrange("p (c u) k -> p c k u", u=HALVES_OF_PASS),
                     )
-                    if a < BLOCKS_PER_STREAM:
-                        step(s * BLOCKS_PER_STREAM + a)
-                if s > 0:
-                    quantise_stream(s - 1)
-            quantise_stream(STREAMS - 1)
-            bias_cols = work.tile([P, P], BF16, name="bias_cols", tag="work")
-            nc.tensor.transpose(bias_cols[:], bias_rows[:], ident[:])
-            nc.vector.tensor_copy(out=gate_bias[:], in_=bias_cols[:, :CHUNKS])
 
-            for i in range(PASSES, n_blocks + 1):
+            for what, which in HEAD:
+                if what == "load":
+                    load_stream(which)
+                else:
+                    {"b": step, "s": do_stream, "q": quantise_stream}[what](which)
+            first_step = 1 + max(w for what, w in HEAD if what == "b")
+            bias_cols = work.tile([P, P], F32, name="bias_cols", tag="work")
+            nc.tensor.transpose(bias_cols[:], bias_rows[:].bitcast(F32), ident_words[:])
+            nc.vector.tensor_copy(out=gate_bias[:], in_=bias_cols[:].bitcast(BF16)[:, :CHUNKS])
+
+            for i in range(first_step, n_blocks + 1):
                 step(i)
                 if i + LOOKAHEAD == n_blocks:
                     nc.sync.dma_start(out=x_sb[:], in_=x_rows.rearrange("(a p) d -> p a d", p=P))
                     nc.sync.dma_start(out=ln_bias_row[:1, :], in_=ln_mem_b.unsqueeze(0))
                     nc.sync.dma_start(out=proj_bias[:], in_=outproj_b.partition_broadcast(P))
 
+        assert chunks["left"] == CHUNKS and chunks["projected"] == PASSES, chunks
         tail = ctx.enter_context(tc.tile_pool(name="tail", bufs=1))
         ln_gain = tail.tile([P, D], BF16, name="ln_gain")
         nc.sync.dma_start(out=ln_gain[:], in_=ln_mem_g.partition_broadcast(P))
@@ -303,13 +344,15 @@ def tile_titanstnt_pb_kernel(
         nc.scalar.activation(out=table_out[:], in_=eps[:], func=ACT.Sqrt)
 
         m = {}
+        sums = {}
         neg_mean = {}
         std = {}
         residual = {}
         squares = tail.tile([P, D], BF16, name="squares")
-        for a in range(TOKEN_TILES):
+
+        def add_bias(a):
             m[a] = tail.tile([P, D], F32, name="m%d" % a)
-            sums = tail.tile([P, HALVES], F32, name="sums%d" % a)
+            sums[a] = tail.tile([P, HALVES], F32, name="sums%d" % a)
             for h in range(HALVES):
                 cols = slice(h * BANK, (h + 1) * BANK)
                 nc.vector.scalar_tensor_tensor(
@@ -319,13 +362,20 @@ def tile_titanstnt_pb_kernel(
                     in1=proj_bias[:, cols],
                     op0=ALU.mult,
                     op1=ALU.add,
-                    accum_out=sums[:, h : h + 1],
+                    accum_out=sums[a][:, h : h + 1],
                 )
+            for h in range(HALVES):
+                cols = slice(h * BANK, (h + 1) * BANK)
+                residual[a, h] = acc_pool.tile([P, BANK], F32, name="residual%d%d" % (a, h), tag="bank%d%d" % (a, h))
+                nc.tensor.matmul(out=residual[a, h][:], lhsT=ident[:], rhs=x_sb[:, a, cols], start=True, stop=False)
+                nc.tensor.matmul(out=residual[a, h][:], lhsT=ones[:], rhs=ln_bias_row[:, cols], start=False, stop=True)
+
+        def find_deviation(a):
             neg_mean[a] = tail.tile([P, 1], F32, name="neg_mean%d" % a)
             nc.vector.tensor_scalar(
                 out=neg_mean[a][:],
-                in0=sums[:, 0:1],
-                scalar1=sums[:, 1:2],
+                in0=sums[a][:, 0:1],
+                scalar1=sums[a][:, 1:2],
                 scalar2=-1.0 / D,
                 op0=ALU.add,
                 op1=ALU.mult,
@@ -336,16 +386,13 @@ def tile_titanstnt_pb_kernel(
             )
             std[a] = tail.tile([P, 1], F32, name="std%d" % a)
             nc.scalar.activation(out=std[a][:], in_=sum_sq[:], func=ACT.Sqrt, bias=eps[:], scale=1.0 / D)
-            for h in range(HALVES):
-                cols = slice(h * BANK, (h + 1) * BANK)
-                residual[a, h] = acc_pool.tile([P, BANK], F32, name="residual%d%d" % (a, h), tag="bank%d%d" % (a, h))
-                nc.tensor.matmul(out=residual[a, h][:], lhsT=ident[:], rhs=x_sb[:, a, cols], start=True, stop=False)
-                nc.tensor.matmul(out=residual[a, h][:], lhsT=ones[:], rhs=ln_bias_row[:, cols], start=False, stop=True)
 
-        for a in range(TOKEN_TILES):
+        def apply_gain(a):
             nc.vector.scalar_tensor_tensor(
                 out=m[a][:], in0=m[a][:], scalar=neg_mean[a][:], in1=ln_gain[:], op0=ALU.add, op1=ALU.mult
             )
+
+        def finish(a):
             rstd = tail.tile([P, 1], F32, name="rstd%d" % a)
             nc.vector.reciprocal(out=rstd[:], in_=std[a][:])
             for h in range(HALVES):
@@ -354,3 +401,16 @@ def tile_titanstnt_pb_kernel(
                     out=m[a][:, cols], in0=m[a][:, cols], scalar=rstd[:], in1=residual[a, h][:], op0=ALU.mult, op1=ALU.add
                 )
                 nc.sync.dma_start(out=out_rows[a * P : (a + 1) * P, cols], in_=m[a][:, cols])
+
+        add_bias(0)
+        add_bias(1)
+        find_deviation(0)
+        add_bias(2)
+        find_deviation(1)
+        apply_gain(0)
+        find_deviation(2)
+        apply_gain(1)
+        finish(0)
+        apply_gain(2)
+        finish(1)
+        finish(2)

@@ -273,6 +273,8 @@ def tile_titanstnt_pb_kernel(
             grouped_pool = stage.enter_context(tc.tile_pool(name="grouped_pool", bufs=3))
             acts = stage.enter_context(tc.tile_pool(name="acts", bufs=1))
 
+            nc.vector.memset(table_in[:], 0.0)
+            nc.scalar.activation(out=table_out[:], in_=table_in[:], func=ACT.Sigmoid)
             act_rows = {}
 
             def load_stream(s):
@@ -285,12 +287,7 @@ def tile_titanstnt_pb_kernel(
 
             make_identity(nc, ident_words[:])
             nc.vector.tensor_copy(out=ident[:], in_=ident_words[:])
-            bias_rows = acts.tile([P, PAIR * P], BF16, name="bias_rows")
-            nc.vector.memset(bias_rows[:], 0.0)
-            nc.scalar.dma_start(out=bias_rows[: CHUNKS // PAIR, :], in_=gate_b.rearrange("(r p) -> r p", p=PAIR * P))
             nc.vector.memset(eps[:], EPS)
-            nc.vector.memset(table_in[:], 0.0)
-            nc.scalar.activation(out=table_out[:], in_=table_in[:], func=ACT.Sigmoid)
             nc.vector.memset(ones[:], 1.0)
             nc.vector.memset(ln_bias_row[:], 0.0)
 
@@ -322,6 +319,9 @@ def tile_titanstnt_pb_kernel(
             for what, which in HEAD:
                 if what == "load":
                     load_stream(which)
+                    bias_rows = acts.tile([P, PAIR * P], BF16, name="bias_rows")
+                    nc.vector.memset(bias_rows[:], 0.0)
+                    nc.sync.dma_start(out=bias_rows[: CHUNKS // PAIR, :], in_=gate_b.rearrange("(r p) -> r p", p=PAIR * P))
                 else:
                     {"b": step, "s": do_stream, "q": quantise_stream}[what](which)
             first_step = 1 + max(w for what, w in HEAD if what == "b")

@@ -45,6 +45,10 @@ PAIR = 2
 HALVES_OF_PASS = 2
 RUN = 4
 
+FAN_BANK = 256
+FANS = lambda i: 0
+VEC = lambda i, n: (576 if i < 6 else 512) - 64 * n
+FAN_LATE = False
 LOOKAHEAD = 4
 Z_BANKS = 2
 BLOCKS_PER_STREAM = PASSES // STREAMS
@@ -103,12 +107,13 @@ def tile_titanstnt_pb_kernel(
         proj_scales = keep.tile([P, PASSES, D], U8, name="proj_scales", align_bytes=64)
         x_sb = keep.tile([P, TOKEN_TILES, D], BF16, name="x_sb")
         proj_bias = keep.tile([P, D], BF16, name="proj_bias")
+        ln_gain = keep.tile([P, D], BF16, name="ln_gain")
         ones = keep.tile([P, P], BF16, name="ones")
         ln_bias_row = keep.tile([P, D], BF16, name="ln_bias_row")
-        acc = [
-            [acc_pool.tile([P, BANK], F32, name="acc%d%d" % (a, h), tag="bank%d%d" % (a, h)) for h in range(HALVES)]
-            for a in range(TOKEN_TILES)
-        ]
+        acc = {}
+        bank_tags = ["bank%d%d" % (a, h) for a in range(TOKEN_TILES) for h in range(HALVES)]
+        fanned = {}
+        fan_count = {"n": 0}
 
         raw = {}
         grouped = {}
@@ -148,6 +153,32 @@ def tile_titanstnt_pb_kernel(
                 in_=src[:, :, first:last].rearrange("p t (c i e) -> p e c t i", i=RUN, e=PAIR),
             )
 
+        def fan_copies(i):
+            for b in range(FANS(i)):
+                first = BLOCK_COLS - (b + 1) * FAN_BANK
+                nc.scalar.copy(
+                    out=grouped[i][:].rearrange("p (e m) t -> p e m t", e=PAIR)[
+                        :, :, first // PAIR : (first + FAN_BANK) // PAIR, :
+                    ],
+                    in_=fanned[i, b][:],
+                )
+
+        def fan_block(i):
+            for b in range(FANS(i)):
+                fanned[i, b] = acc_pool.tile(
+                    [P, PAIR, P, PACK], BF16, name="fanned", tag=bank_tags[fan_count["n"] % len(bank_tags)]
+                )
+                fan_count["n"] += 1
+                first = BLOCK_COLS - (b + 1) * FAN_BANK
+                for t in range(PACK):
+                    nc.tensor.matmul(
+                        out=fanned[i, b][:, :, :, t].rearrange("p e m -> p m e"),
+                        lhsT=ident[:],
+                        rhs=raw[i][:, t, first : first + FAN_BANK].rearrange("p (m e) -> p m e", e=PAIR),
+                        start=True,
+                        stop=True,
+                    )
+
         def regroup_block(i):
             grouped[i] = grouped_pool.tile(
                 [P, BLOCK_COLS, PACK], BF16, name="grouped", tag="grouped", align_bytes=64
@@ -156,8 +187,12 @@ def tile_titanstnt_pb_kernel(
                 regroup(nc.vector.tensor_copy, grouped[i][:, :VEC_COLS, :], raw[i][:, :, :VEC_COLS])
                 regroup(nc.scalar.copy, grouped[i][:, VEC_COLS:, :], raw[i][:, :, VEC_COLS:])
             else:
-                regroup_gate(nc.vector.tensor_copy, grouped[i], raw[i], 0, VEC_COLS)
-                regroup_gate(nc.scalar.copy, grouped[i], raw[i], VEC_COLS, BLOCK_COLS)
+                n = FANS(i)
+                vec_cols = VEC(i, n)
+                last = BLOCK_COLS - n * FAN_BANK
+                regroup_gate(nc.vector.tensor_copy, grouped[i], raw[i], 0, vec_cols)
+                if vec_cols < last:
+                    regroup_gate(nc.scalar.copy, grouped[i], raw[i], vec_cols, last)
 
         def quantise_block(i):
             kind, wide, c = blocks[i]
@@ -223,12 +258,15 @@ def tile_titanstnt_pb_kernel(
 
         def project(g):
             for a in range(TOKEN_TILES):
+                if g == 0:
+                    for h in range(HALVES):
+                        acc[a, h] = acc_pool.tile([P, BANK], F32, name="acc%d%d" % (a, h), tag="bank%d%d" % (a, h))
                 grp, tile_in_group = divmod(a, TILES_IN_FIRST_GROUP)
                 toks = slice(tile_in_group * P, (tile_in_group + 1) * P)
                 for h in range(HALVES):
                     cols = slice(h * BANK, (h + 1) * BANK)
                     nc.tensor.matmul_mx(
-                        out=acc[a][h][:],
+                        out=acc[a, h][:],
                         lhsT=gated_codes[grp][:, g, toks].bitcast(FP8X4),
                         lhsT_scale=gated_scales[grp][:, g, toks],
                         rhs=proj_codes[:, g, cols].bitcast(FP8X4),
@@ -245,12 +283,17 @@ def tile_titanstnt_pb_kernel(
             advance = min(advance, MAX_ADV)
             first_left = chunks["left"]
             chunks["left"] = max(first_left, min(chunks["entered"], chunks["entered"] + advance - Z_BANKS + EAGER))
-            if i >= n_blocks:
-                chunks["left"] = chunks["entered"]
+            if chunks["entered"] == CHUNKS:
+                chunks["left"] = CHUNKS
             for e in range(first_left, chunks["left"]):
                 gate_sigmoid(e)
+            if FAN_LATE and i >= 1:
+                fan_copies(i - 1)
             if i < n_blocks:
+                fan_block(i)
                 regroup_block(i)
+                if not FAN_LATE:
+                    fan_copies(i)
             if i + LOOKAHEAD < n_blocks:
                 load_block(i + LOOKAHEAD)
             if i >= 1:
@@ -279,7 +322,7 @@ def tile_titanstnt_pb_kernel(
 
             def load_stream(s):
                 for a in range(TOKEN_TILES):
-                    act_rows[s, a] = acts.tile([P, D], BF16, name="act_rows%d%d" % (s, a))
+                    act_rows[s, a] = acts.tile([P, D], BF16, name="act_rows", tag="act_rows%d" % a, bufs=2)
                     nc.sync.dma_start(out=act_rows[s, a][:], in_=streams[s][a * P : (a + 1) * P, :])
 
             for what, which in HEAD_LOADS:
@@ -335,11 +378,10 @@ def tile_titanstnt_pb_kernel(
                     nc.sync.dma_start(out=x_sb[:], in_=x_rows.rearrange("(a p) d -> p a d", p=P))
                     nc.sync.dma_start(out=ln_bias_row[:1, :], in_=ln_mem_b.unsqueeze(0))
                     nc.sync.dma_start(out=proj_bias[:], in_=outproj_b.partition_broadcast(P))
+                    nc.sync.dma_start(out=ln_gain[:], in_=ln_mem_g.partition_broadcast(P))
 
         assert chunks["left"] == CHUNKS and chunks["projected"] == PASSES, chunks
         tail = ctx.enter_context(tc.tile_pool(name="tail", bufs=1))
-        ln_gain = tail.tile([P, D], BF16, name="ln_gain")
-        nc.sync.dma_start(out=ln_gain[:], in_=ln_mem_g.partition_broadcast(P))
 
         nc.scalar.activation(out=table_out[:], in_=eps[:], func=ACT.Sqrt)
 
@@ -347,6 +389,7 @@ def tile_titanstnt_pb_kernel(
         sums = {}
         neg_mean = {}
         std = {}
+        rstd = {}
         residual = {}
         squares = tail.tile([P, D], BF16, name="squares")
 
@@ -357,7 +400,7 @@ def tile_titanstnt_pb_kernel(
                 cols = slice(h * BANK, (h + 1) * BANK)
                 nc.vector.scalar_tensor_tensor(
                     out=m[a][:, cols],
-                    in0=acc[a][h][:],
+                    in0=acc[a, h][:],
                     scalar=1.0,
                     in1=proj_bias[:, cols],
                     op0=ALU.mult,
@@ -392,13 +435,15 @@ def tile_titanstnt_pb_kernel(
                 out=m[a][:], in0=m[a][:], scalar=neg_mean[a][:], in1=ln_gain[:], op0=ALU.add, op1=ALU.mult
             )
 
+        def invert(a):
+            rstd[a] = tail.tile([P, 1], F32, name="rstd%d" % a)
+            nc.vector.reciprocal(out=rstd[a][:], in_=std[a][:])
+
         def finish(a):
-            rstd = tail.tile([P, 1], F32, name="rstd%d" % a)
-            nc.vector.reciprocal(out=rstd[:], in_=std[a][:])
             for h in range(HALVES):
                 cols = slice(h * BANK, (h + 1) * BANK)
                 nc.vector.scalar_tensor_tensor(
-                    out=m[a][:, cols], in0=m[a][:, cols], scalar=rstd[:], in1=residual[a, h][:], op0=ALU.mult, op1=ALU.add
+                    out=m[a][:, cols], in0=m[a][:, cols], scalar=rstd[a][:], in1=residual[a, h][:], op0=ALU.mult, op1=ALU.add
                 )
                 nc.sync.dma_start(out=out_rows[a * P : (a + 1) * P, cols], in_=m[a][:, cols])
 
@@ -410,7 +455,10 @@ def tile_titanstnt_pb_kernel(
         apply_gain(0)
         find_deviation(2)
         apply_gain(1)
-        finish(0)
+        invert(0)
         apply_gain(2)
+        finish(0)
+        invert(1)
+        invert(2)
         finish(1)
         finish(2)

@@ -41,6 +41,8 @@ CHUNKS = C // P
 CHUNKS_PER_WIDE = BLOCK_COLS // P
 PROJ_EARLY = 1
 VEC_COLS = 512
+HALF_COLS = (slice(0, 512), slice(512, 1024))
+LAST_CUTS = ((0, 256, 512), (512, 768, 1024))
 PAIR = 2
 HALVES_OF_PASS = 2
 RUN = 4
@@ -132,7 +134,7 @@ def tile_titanstnt_pb_kernel(
 
         def load_block(i):
             raw[i] = raw_pool.tile([P, PACK, BLOCK_COLS], BF16, name="raw", tag="raw")
-            for cols in (slice(0, VEC_COLS), slice(VEC_COLS, BLOCK_COLS)) if i == 0 else (slice(0, BLOCK_COLS),):
+            for cols in HALF_COLS if i in (0, n_blocks - 1) else (slice(0, BLOCK_COLS),):
                 for u in range(HALVES_OF_PASS):
                     nc.sync.dma_start(
                         out=raw[i][:, PAIR * u : PAIR * (u + 1), cols],
@@ -184,8 +186,9 @@ def tile_titanstnt_pb_kernel(
                 [P, BLOCK_COLS, PACK], BF16, name="grouped", tag="grouped", align_bytes=64
             )
             if blocks[i][0] == "proj":
-                regroup(nc.vector.tensor_copy, grouped[i][:, :VEC_COLS, :], raw[i][:, :, :VEC_COLS])
-                regroup(nc.scalar.copy, grouped[i][:, VEC_COLS:, :], raw[i][:, :, VEC_COLS:])
+                for first, vec_cols, last in LAST_CUTS if i == n_blocks - 1 else ((0, VEC_COLS, BLOCK_COLS),):
+                    regroup(nc.vector.tensor_copy, grouped[i][:, first:vec_cols, :], raw[i][:, :, first:vec_cols])
+                    regroup(nc.scalar.copy, grouped[i][:, vec_cols:last, :], raw[i][:, :, vec_cols:last])
             else:
                 n = FANS(i)
                 vec_cols = VEC(i, n)
@@ -207,9 +210,12 @@ def tile_titanstnt_pb_kernel(
                 codes, scales = gate_codes[wide][:, c, :], gate_scales[wide][:, c, :]
             else:
                 codes, scales = proj_codes[:, c, :], proj_scales[:, c, :]
-            nc.vector.quantize_mx(
-                out=codes.bitcast(FP8X4), scales=scales, in_=grouped[i][:].rearrange("p n t -> p (n t)")
-            )
+            for cols in HALF_COLS if i == n_blocks - 1 else (slice(0, BLOCK_COLS),):
+                nc.vector.quantize_mx(
+                    out=codes[:, cols].bitcast(FP8X4),
+                    scales=scales[:, cols],
+                    in_=grouped[i][:, cols, :].rearrange("p n t -> p (n t)"),
+                )
 
         def gate_matmuls(e):
             wide, piece = divmod(e, CHUNKS_PER_WIDE)
@@ -244,9 +250,9 @@ def tile_titanstnt_pb_kernel(
                     gating.tile([P, count, PACK], BF16, name="gated%d" % grp, tag="gated%d" % grp, align_bytes=64)
                 )
                 nc.vector.tensor_tensor(
-                    out=gated[grp][:],
-                    in0=gate[g][:, :, first : first + count].rearrange("p t k -> p k t"),
-                    in1=act_grouped[grp][:, g, :, :],
+                    out=gated[grp][:].rearrange("p (c i) t -> p c t i", i=RUN),
+                    in0=gate[g][:, :, first : first + count].rearrange("p t (c i) -> p c t i", i=RUN),
+                    in1=act_grouped[grp][:, g, :, :].rearrange("p (c i) t -> p c t i", i=RUN),
                     op=ALU.mult,
                 )
             for grp in range(len(TOKEN_GROUPS)):
@@ -257,23 +263,24 @@ def tile_titanstnt_pb_kernel(
                 )
 
         def project(g):
-            for a in range(TOKEN_TILES):
+            pairs = [(a, h) for a in range(TOKEN_TILES) for h in range(HALVES)]
+            if g == PASSES - 1:
+                pairs = sorted(pairs, key=lambda pair: pair[1])
+            for a, h in pairs:
                 if g == 0:
-                    for h in range(HALVES):
-                        acc[a, h] = acc_pool.tile([P, BANK], F32, name="acc%d%d" % (a, h), tag="bank%d%d" % (a, h))
+                    acc[a, h] = acc_pool.tile([P, BANK], F32, name="acc%d%d" % (a, h), tag="bank%d%d" % (a, h))
                 grp, tile_in_group = divmod(a, TILES_IN_FIRST_GROUP)
                 toks = slice(tile_in_group * P, (tile_in_group + 1) * P)
-                for h in range(HALVES):
-                    cols = slice(h * BANK, (h + 1) * BANK)
-                    nc.tensor.matmul_mx(
-                        out=acc[a, h][:],
-                        lhsT=gated_codes[grp][:, g, toks].bitcast(FP8X4),
-                        lhsT_scale=gated_scales[grp][:, g, toks],
-                        rhs=proj_codes[:, g, cols].bitcast(FP8X4),
-                        rhs_scale=proj_scales[:, g, cols],
-                        start=(g == 0),
-                        stop=(g == PASSES - 1),
-                    )
+                cols = slice(h * BANK, (h + 1) * BANK)
+                nc.tensor.matmul_mx(
+                    out=acc[a, h][:],
+                    lhsT=gated_codes[grp][:, g, toks].bitcast(FP8X4),
+                    lhsT_scale=gated_scales[grp][:, g, toks],
+                    rhs=proj_codes[:, g, cols].bitcast(FP8X4),
+                    rhs_scale=proj_scales[:, g, cols],
+                    start=(g == 0),
+                    stop=(g == PASSES - 1),
+                )
 
         def step(i):
             if i >= 1 and blocks[i - 1][0] == "gate" and blocks[i - 1][2] == PASSES - 1:

@@ -45,6 +45,7 @@ HALF_COLS = (slice(0, 512), slice(512, 1024))
 LAST_CUTS = ((0, 256, 512), (512, 768, 1024))
 PAIR = 2
 HALVES_OF_PASS = 2
+LINE = 8
 RUN = 4
 
 FAN_BANK = 256
@@ -143,8 +144,8 @@ def tile_titanstnt_pb_kernel(
 
         def regroup(copy, dst, src):
             copy(
-                out=dst.rearrange("p (c i) t -> p c t i", i=RUN),
-                in_=src.rearrange("p t (c i) -> p c t i", i=RUN),
+                out=dst.rearrange("p (c i) t -> p c t i", i=LINE),
+                in_=src.rearrange("p t (c i) -> p c t i", i=LINE),
             )
 
         def regroup_gate(copy, dst, src, first, last):

@@ -33,7 +33,6 @@ HALVES = D // BANK
 EPS = 1e-5
 
 TOKEN_GROUPS = ((0, 256), (256, 128))
-TILES_IN_FIRST_GROUP = 2
 
 BLOCK_COLS = 1024
 WIDE = C // BLOCK_COLS
@@ -45,6 +44,7 @@ HALF_COLS = (slice(0, 512), slice(512, 1024))
 LAST_CUTS = ((0, 256, 512), (512, 768, 1024))
 PAIR = 2
 HALVES_OF_PASS = 2
+BY_TENSOR = ((0, 0), (0, 1), (1, 0))
 LINE = 8
 RUN = 4
 
@@ -86,26 +86,11 @@ def tile_titanstnt_pb_kernel(
         eps = keep.tile([P, 1], F32, name="eps")
         table_in = keep.tile([P, 1], F32, name="table_in")
         table_out = keep.tile([P, 1], F32, name="table_out")
-        act_grouped = [
-            keep.tile([P, PASSES, count, PACK], BF16, name="act_grouped%d" % grp, align_bytes=64)
-            for grp, (first, count) in enumerate(TOKEN_GROUPS)
-        ]
-        act_codes = [
-            keep.tile([P, PASSES, count], U32, name="act_codes%d" % grp, align_bytes=64)
-            for grp, (first, count) in enumerate(TOKEN_GROUPS)
-        ]
-        act_scales = [
-            keep.tile([P, PASSES, count], U8, name="act_scales%d" % grp, align_bytes=64)
-            for grp, (first, count) in enumerate(TOKEN_GROUPS)
-        ]
-        gated_codes = [
-            keep.tile([P, PASSES, count], U32, name="gated_codes%d" % grp, align_bytes=64)
-            for grp, (first, count) in enumerate(TOKEN_GROUPS)
-        ]
-        gated_scales = [
-            keep.tile([P, PASSES, count], U8, name="gated_scales%d" % grp, align_bytes=64)
-            for grp, (first, count) in enumerate(TOKEN_GROUPS)
-        ]
+        act_grouped = keep.tile([P, PASSES, TOKENS, PACK], BF16, name="act_grouped", align_bytes=64)
+        act_codes = keep.tile([P, PASSES, TOKENS], U32, name="act_codes", align_bytes=64)
+        act_scales = keep.tile([P, PASSES, TOKENS], U8, name="act_scales", align_bytes=64)
+        gated_codes = keep.tile([P, PASSES, TOKENS], U32, name="gated_codes", align_bytes=64)
+        gated_scales = keep.tile([P, PASSES, TOKENS], U8, name="gated_scales", align_bytes=64)
         proj_codes = keep.tile([P, PASSES, D], U32, name="proj_codes", align_bytes=64)
         proj_scales = keep.tile([P, PASSES, D], U8, name="proj_scales", align_bytes=64)
         x_sb = keep.tile([P, TOKEN_TILES, D], BF16, name="x_sb")
@@ -124,6 +109,8 @@ def tile_titanstnt_pb_kernel(
         gate_scales = {}
         z = {}
         gate = {}
+        gated = {}
+        pending = []
         chunks = {"entered": 0, "left": 0, "weights": 0, "gated": 0, "projected": 0, "ready": 0}
 
         def block_rows(i):
@@ -212,6 +199,8 @@ def tile_titanstnt_pb_kernel(
             else:
                 codes, scales = proj_codes[:, c, :], proj_scales[:, c, :]
             for cols in HALF_COLS if i == n_blocks - 1 else (slice(0, BLOCK_COLS),):
+                if i == n_blocks - 1 and cols == HALF_COLS[-1]:
+                    quantise_gated()
                 nc.vector.quantize_mx(
                     out=codes[:, cols].bitcast(FP8X4),
                     scales=scales[:, cols],
@@ -230,11 +219,14 @@ def tile_titanstnt_pb_kernel(
                         out=z[e][:, first : first + count],
                         lhsT=gate_codes[wide][:, c, cols].bitcast(FP8X4),
                         lhsT_scale=gate_scales[wide][:, c, cols],
-                        rhs=act_codes[grp][:, c, :].bitcast(FP8X4),
-                        rhs_scale=act_scales[grp][:, c, :],
+                        rhs=act_codes[:, c, first : first + count].bitcast(FP8X4),
+                        rhs_scale=act_scales[:, c, first : first + count],
                         start=(c == 0),
                         stop=(c == PASSES - 1),
                     )
+
+        def joined(g):
+            return (g // PAIR * PAIR, PAIR) if g < PASSES - PAIR else (g, 1)
 
         def gate_sigmoid(e):
             g, t = divmod(e, PACK)
@@ -244,24 +236,38 @@ def tile_titanstnt_pb_kernel(
                 out=gate[g][:, t, :], in_=z[e][:], func=ACT.Sigmoid, bias=gate_bias[:, e : e + 1], scale=1.0
             )
 
-        def gate_product(g):
-            gated = []
-            for grp, (first, count) in enumerate(TOKEN_GROUPS):
-                gated.append(
-                    gating.tile([P, count, PACK], BF16, name="gated%d" % grp, tag="gated%d" % grp, align_bytes=64)
-                )
-                nc.vector.tensor_tensor(
-                    out=gated[grp][:].rearrange("p (c i) t -> p c t i", i=RUN),
-                    in0=gate[g][:, :, first : first + count].rearrange("p t (c i) -> p c t i", i=RUN),
-                    in1=act_grouped[grp][:, g, :, :].rearrange("p (c i) t -> p c t i", i=RUN),
-                    op=ALU.mult,
-                )
-            for grp in range(len(TOKEN_GROUPS)):
+        def quantise_runs(codes, scales, values):
+            words = codes.shape[1]
+            for run in (slice(0, 2 * words // 3), slice(2 * words // 3, words)):
                 nc.vector.quantize_mx(
-                    out=gated_codes[grp][:, g, :].bitcast(FP8X4),
-                    scales=gated_scales[grp][:, g, :],
-                    in_=gated[grp][:].rearrange("p k t -> p (k t)"),
+                    out=codes[:, run].bitcast(FP8X4),
+                    scales=scales[:, run],
+                    in_=values[:, run, :].rearrange("p w t -> p (w t)"),
                 )
+
+        def gate_product(g):
+            first, count = joined(g)
+            if g == first:
+                gated[first] = gating.tile([P, count, TOKENS, PACK], BF16, name="gated", tag="gated", align_bytes=64)
+            nc.vector.tensor_tensor(
+                out=gated[first][:, g - first, :, :].rearrange("p (c i) t -> p c t i", i=RUN),
+                in0=gate[g][:].rearrange("p t (c i) -> p c t i", i=RUN),
+                in1=act_grouped[:, g, :, :].rearrange("p (c i) t -> p c t i", i=RUN),
+                op=ALU.mult,
+            )
+            if g == first + count - 1:
+                pending.append(first)
+
+        def quantise_gated():
+            while pending:
+                first, count = joined(pending.pop(0))
+                span = slice(first, first + count)
+                quantise_runs(
+                    gated_codes[:, span, :].rearrange("p c k -> p (c k)"),
+                    gated_scales[:, span, :].rearrange("p c k -> p (c k)"),
+                    gated[first][:].rearrange("p c k t -> p (c k) t"),
+                )
+                chunks["gated"] += count
 
         def project(g):
             pairs = [(a, h) for a in range(TOKEN_TILES) for h in range(HALVES)]
@@ -270,13 +276,12 @@ def tile_titanstnt_pb_kernel(
             for a, h in pairs:
                 if g == 0:
                     acc[a, h] = acc_pool.tile([P, BANK], F32, name="acc%d%d" % (a, h), tag="bank%d%d" % (a, h))
-                grp, tile_in_group = divmod(a, TILES_IN_FIRST_GROUP)
-                toks = slice(tile_in_group * P, (tile_in_group + 1) * P)
+                toks = slice(a * P, (a + 1) * P)
                 cols = slice(h * BANK, (h + 1) * BANK)
                 nc.tensor.matmul_mx(
                     out=acc[a, h][:],
-                    lhsT=gated_codes[grp][:, g, toks].bitcast(FP8X4),
-                    lhsT_scale=gated_scales[grp][:, g, toks],
+                    lhsT=gated_codes[:, g, toks].bitcast(FP8X4),
+                    lhsT_scale=gated_scales[:, g, toks],
                     rhs=proj_codes[:, g, cols].bitcast(FP8X4),
                     rhs_scale=proj_scales[:, g, cols],
                     start=(g == 0),
@@ -304,12 +309,13 @@ def tile_titanstnt_pb_kernel(
                     fan_copies(i)
             if i + LOOKAHEAD < n_blocks:
                 load_block(i + LOOKAHEAD)
+            if i < n_blocks:
+                quantise_gated()
             if i >= 1:
                 quantise_block(i - 1)
             for e in range(first_left, chunks["left"]):
                 if e % PACK == PACK - 1:
                     gate_product(e // PACK)
-                    chunks["gated"] += 1
             for e in range(chunks["entered"], chunks["entered"] + advance):
                 gate_matmuls(e)
             chunks["entered"] += advance
@@ -344,12 +350,11 @@ def tile_titanstnt_pb_kernel(
 
             def quantise_stream(s):
                 passes = slice(s * PASSES_PER_STREAM, (s + 1) * PASSES_PER_STREAM)
-                for grp in range(len(TOKEN_GROUPS)):
-                    nc.vector.quantize_mx(
-                        out=act_codes[grp][:, passes, :].rearrange("p c k -> p (c k)").bitcast(FP8X4),
-                        scales=act_scales[grp][:, passes, :].rearrange("p c k -> p (c k)"),
-                        in_=act_grouped[grp][:, passes, :, :].rearrange("p c k t -> p (c k t)"),
-                    )
+                quantise_runs(
+                    act_codes[:, passes, :].rearrange("p c k -> p (c k)"),
+                    act_scales[:, passes, :].rearrange("p c k -> p (c k)"),
+                    act_grouped[:, passes, :, :].rearrange("p c k t -> p (c k) t"),
+                )
 
             def do_stream(s):
                 passes = slice(s * PASSES_PER_STREAM, (s + 1) * PASSES_PER_STREAM)
@@ -359,11 +364,10 @@ def tile_titanstnt_pb_kernel(
                         nc.tensor.transpose(
                             turned[:, j, :], act_rows[s, a][:].bitcast(F32)[:, j * P : (j + 1) * P], ident_words[:]
                         )
-                    grp, tile_in_group = divmod(a, TILES_IN_FIRST_GROUP)
-                    toks = slice(tile_in_group * P, (tile_in_group + 1) * P)
+                    toks = slice(a * P, (a + 1) * P)
                     copy = nc.vector.tensor_copy if a in ACT_VEC else nc.scalar.copy
                     copy(
-                        out=act_grouped[grp][:, passes, toks, :].bitcast(F32),
+                        out=act_grouped[:, passes, toks, :].bitcast(F32),
                         in_=turned[:].rearrange("p (c u) k -> p c k u", u=HALVES_OF_PASS),
                     )
 
@@ -391,37 +395,41 @@ def tile_titanstnt_pb_kernel(
         assert chunks["left"] == CHUNKS and chunks["projected"] == PASSES, chunks
         tail = ctx.enter_context(tc.tile_pool(name="tail", bufs=1))
 
-        nc.scalar.activation(out=table_out[:], in_=eps[:], func=ACT.Sqrt)
+        nc.scalar.activation(out=table_out[:], in_=eps[:], func=ACT.Abs_reciprocal_sqrt)
 
         m = {}
+        scaled = {}
         sums = {}
         neg_mean = {}
-        std = {}
         rstd = {}
+        diag = {}
         residual = {}
         squares = tail.tile([P, D], BF16, name="squares")
 
-        def add_bias(a):
-            m[a] = tail.tile([P, D], F32, name="m%d" % a)
-            sums[a] = tail.tile([P, HALVES], F32, name="sums%d" % a)
-            for h in range(HALVES):
-                cols = slice(h * BANK, (h + 1) * BANK)
-                nc.vector.scalar_tensor_tensor(
-                    out=m[a][:, cols],
-                    in0=acc[a, h][:],
-                    scalar=1.0,
-                    in1=proj_bias[:, cols],
-                    op0=ALU.mult,
-                    op1=ALU.add,
-                    accum_out=sums[a][:, h : h + 1],
-                )
-            for h in range(HALVES):
-                cols = slice(h * BANK, (h + 1) * BANK)
-                residual[a, h] = acc_pool.tile([P, BANK], F32, name="residual%d%d" % (a, h), tag="bank%d%d" % (a, h))
-                nc.tensor.matmul(out=residual[a, h][:], lhsT=ident[:], rhs=x_sb[:, a, cols], start=True, stop=False)
-                nc.tensor.matmul(out=residual[a, h][:], lhsT=ones[:], rhs=ln_bias_row[:, cols], start=False, stop=True)
+        def add_bias(a, h):
+            if h == 0:
+                m[a] = tail.tile([P, D], F32, name="m%d" % a)
+                sums[a] = tail.tile([P, HALVES], F32, name="sums%d" % a)
+            cols = slice(h * BANK, (h + 1) * BANK)
+            nc.vector.scalar_tensor_tensor(
+                out=m[a][:, cols],
+                in0=acc[a, h][:],
+                scalar=1.0,
+                in1=proj_bias[:, cols],
+                op0=ALU.mult,
+                op1=ALU.add,
+                accum_out=sums[a][:, h : h + 1],
+            )
 
-        def find_deviation(a):
+        def open_residual(a, h):
+            cols = slice(h * BANK, (h + 1) * BANK)
+            residual[a, h] = acc_pool.tile([P, BANK], F32, name="residual%d%d" % (a, h), tag="bank%d%d" % (a, h))
+            nc.tensor.matmul(out=residual[a, h][:], lhsT=ident[:], rhs=x_sb[:, a, cols], start=True, stop=False)
+            nc.tensor.matmul(
+                out=residual[a, h][:], lhsT=ones[:], rhs=ln_bias_row[:, cols], start=False, stop=(a, h) not in BY_TENSOR
+            )
+
+        def find_mean(a):
             neg_mean[a] = tail.tile([P, 1], F32, name="neg_mean%d" % a)
             nc.vector.tensor_scalar(
                 out=neg_mean[a][:],
@@ -431,42 +439,79 @@ def tile_titanstnt_pb_kernel(
                 op0=ALU.add,
                 op1=ALU.mult,
             )
+
+        def find_deviation(a):
             sum_sq = tail.tile([P, 1], F32, name="sum_sq%d" % a)
             nc.scalar.activation(
                 out=squares[:], in_=m[a][:], func=ACT.Square, bias=neg_mean[a][:], scale=1.0, accum_out=sum_sq[:]
             )
-            std[a] = tail.tile([P, 1], F32, name="std%d" % a)
-            nc.scalar.activation(out=std[a][:], in_=sum_sq[:], func=ACT.Sqrt, bias=eps[:], scale=1.0 / D)
+            rstd[a] = tail.tile([P, 1], F32, name="rstd%d" % a)
+            nc.scalar.activation(
+                out=rstd[a][:], in_=sum_sq[:], func=ACT.Abs_reciprocal_sqrt, bias=eps[:], scale=1.0 / D
+            )
+            if (a, 0) in BY_TENSOR:
+                diag[a] = tail.tile([P, P], F32, name="diag%d" % a)
+                nc.scalar.activation(out=diag[a][:], in_=ident_words[:], func=ACT.Copy, scale=rstd[a][:])
 
         def apply_gain(a):
+            scaled[a] = tail.tile([P, D], F32, name="scaled%d" % a)
             nc.vector.scalar_tensor_tensor(
-                out=m[a][:], in0=m[a][:], scalar=neg_mean[a][:], in1=ln_gain[:], op0=ALU.add, op1=ALU.mult
+                out=scaled[a][:], in0=m[a][:], scalar=neg_mean[a][:], in1=ln_gain[:], op0=ALU.add, op1=ALU.mult
             )
 
-        def invert(a):
-            rstd[a] = tail.tile([P, 1], F32, name="rstd%d" % a)
-            nc.vector.reciprocal(out=rstd[a][:], in_=std[a][:])
+        def store(a, h):
+            cols = slice(h * BANK, (h + 1) * BANK)
+            nc.sync.dma_start(out=out_rows[a * P : (a + 1) * P, cols], in_=m[a][:, cols])
 
-        def finish(a):
+        def finish_on_vector(a, h):
+            cols = slice(h * BANK, (h + 1) * BANK)
+            nc.vector.scalar_tensor_tensor(
+                out=m[a][:, cols],
+                in0=scaled[a][:, cols],
+                scalar=rstd[a][:],
+                in1=residual[a, h][:],
+                op0=ALU.mult,
+                op1=ALU.add,
+            )
+            store(a, h)
+
+        def finish_on_tensor(a, h):
+            cols = slice(h * BANK, (h + 1) * BANK)
+            nc.tensor.matmul(out=residual[a, h][:], lhsT=diag[a][:], rhs=scaled[a][:, cols], start=False, stop=True)
+
+        def empty(a, h):
+            cols = slice(h * BANK, (h + 1) * BANK)
+            nc.scalar.copy(out=m[a][:, cols], in_=residual[a, h][:])
+            store(a, h)
+
+        def residuals(a):
             for h in range(HALVES):
-                cols = slice(h * BANK, (h + 1) * BANK)
-                nc.vector.scalar_tensor_tensor(
-                    out=m[a][:, cols], in0=m[a][:, cols], scalar=rstd[a][:], in1=residual[a, h][:], op0=ALU.mult, op1=ALU.add
-                )
-                nc.sync.dma_start(out=out_rows[a * P : (a + 1) * P, cols], in_=m[a][:, cols])
+                open_residual(a, h)
 
-        add_bias(0)
-        add_bias(1)
+        add_bias(0, 0)
+        add_bias(0, 1)
+        residuals(0)
+        add_bias(1, 0)
+        find_mean(0)
         find_deviation(0)
-        add_bias(2)
-        find_deviation(1)
+        add_bias(1, 1)
+        residuals(1)
         apply_gain(0)
+        finish_on_tensor(0, 0)
+        find_mean(1)
+        find_deviation(1)
+        empty(0, 0)
+        add_bias(2, 0)
+        add_bias(2, 1)
+        find_mean(2)
         find_deviation(2)
+        finish_on_tensor(0, 1)
+        residuals(2)
         apply_gain(1)
-        invert(0)
+        finish_on_tensor(1, 0)
+        finish_on_vector(1, 1)
+        empty(0, 1)
         apply_gain(2)
-        finish(0)
-        invert(1)
-        invert(2)
-        finish(1)
-        finish(2)
+        finish_on_vector(2, 0)
+        empty(1, 0)
+        finish_on_vector(2, 1)

@@ -39,7 +39,7 @@ WIDE = C // BLOCK_COLS
 CHUNKS = C // P
 CHUNKS_PER_WIDE = BLOCK_COLS // P
 PROJ_EARLY = 1
-VEC_COLS = 512
+VEC_COLS = 480
 HALF_COLS = (slice(0, 512), slice(512, 1024))
 LAST_CUTS = ((0, 256, 512), (512, 768, 1024))
 PAIR = 2
@@ -50,7 +50,7 @@ RUN = 4
 
 FAN_BANK = 256
 FANS = lambda i: 0
-VEC = lambda i, n: (576 if i < 6 else 512) - 64 * n
+VEC = lambda i, n: (576 if i < 6 else 480) - 64 * n
 FAN_LATE = False
 LOOKAHEAD = 4
 Z_BANKS = 2

@@ -21,7 +21,7 @@ WORDS = D // 2
 ACT_VEC = ()
 MAX_ADV = 2
 EAGER = 0
-PACE = lambda i: max(0, (3 * (i - 6)) // 2)
+PACE = lambda h: max(0, (3 * (h - 12)) // 4)
 HEAD_LOADS = (("b",0),("b",1),("s",0),("b",2),("b",3),("s",1))
 HEAD = (("b",0),("b",1),("load",2),("s",0),("b",2),("q",0),("b",3),("s",1),("b",4),("q",1),("b",5),("s",2),("b",6),("q",2))
 STREAMS = 3
@@ -35,11 +35,14 @@ EPS = 1e-5
 TOKEN_GROUPS = ((0, 256), (256, 128))
 
 BLOCK_COLS = 1024
-WIDE = C // BLOCK_COLS
+RANGES = ((0, 1024), (1024, 1024), (2048, 1024))
 CHUNKS = C // P
-CHUNKS_PER_WIDE = BLOCK_COLS // P
+EARLY = range(16, 22)
+LATE_SIGMOIDS = 3
 PROJ_EARLY = 1
 VEC_COLS = 480
+VEC_HEAD = 576
+VEC_PROJ = 416
 HALF_COLS = (slice(0, 512), slice(512, 1024))
 LAST_CUTS = ((0, 256, 512), (512, 768, 1024))
 PAIR = 2
@@ -48,10 +51,6 @@ BY_TENSOR = ((0, 0), (0, 1), (1, 0))
 LINE = 8
 RUN = 4
 
-FAN_BANK = 256
-FANS = lambda i: 0
-VEC = lambda i, n: (576 if i < 6 else 480) - 64 * n
-FAN_LATE = False
 LOOKAHEAD = 4
 Z_BANKS = 2
 BLOCKS_PER_STREAM = PASSES // STREAMS
@@ -67,7 +66,7 @@ def tile_titanstnt_pb_kernel(
     x_rows = x.flatten_outer_dims()
     out_rows = out.flatten_outer_dims()
 
-    gate_blocks = [("gate", wide, c) for wide in range(WIDE) for c in range(PASSES)]
+    gate_blocks = [("gate", wide, c) for wide in range(len(RANGES)) for c in range(PASSES)]
     proj_blocks = [("proj", None, g) for g in range(PASSES)]
     blocks = gate_blocks[:-PASSES] + proj_blocks[:PROJ_EARLY] + gate_blocks[-PASSES:] + proj_blocks[PROJ_EARLY:]
     n_blocks = len(blocks)
@@ -99,9 +98,6 @@ def tile_titanstnt_pb_kernel(
         ones = keep.tile([P, P], BF16, name="ones")
         ln_bias_row = keep.tile([P, D], BF16, name="ln_bias_row")
         acc = {}
-        bank_tags = ["bank%d%d" % (a, h) for a in range(TOKEN_TILES) for h in range(HALVES)]
-        fanned = {}
-        fan_count = {"n": 0}
 
         raw = {}
         grouped = {}
@@ -117,12 +113,14 @@ def tile_titanstnt_pb_kernel(
             kind, wide, c = blocks[i]
             k_rows = slice(c * K_PASS, (c + 1) * K_PASS)
             if kind == "gate":
-                return gate_w[k_rows, wide * BLOCK_COLS : (wide + 1) * BLOCK_COLS]
+                first, width = RANGES[wide]
+                return gate_w[k_rows, first : first + width]
             return outproj_w[k_rows, :]
 
         def load_block(i):
-            raw[i] = raw_pool.tile([P, PACK, BLOCK_COLS], BF16, name="raw", tag="raw")
-            for cols in HALF_COLS if i in (0, n_blocks - 1) else (slice(0, BLOCK_COLS),):
+            width = block_rows(i).shape[1]
+            raw[i] = raw_pool.tile([P, PACK, width], BF16, name="raw", tag="raw")
+            for cols in HALF_COLS if i in (0, n_blocks - 1) else (slice(0, width),):
                 for u in range(HALVES_OF_PASS):
                     nc.sync.dma_start(
                         out=raw[i][:, PAIR * u : PAIR * (u + 1), cols],
@@ -143,62 +141,35 @@ def tile_titanstnt_pb_kernel(
                 in_=src[:, :, first:last].rearrange("p t (c i e) -> p e c t i", i=RUN, e=PAIR),
             )
 
-        def fan_copies(i):
-            for b in range(FANS(i)):
-                first = BLOCK_COLS - (b + 1) * FAN_BANK
-                nc.scalar.copy(
-                    out=grouped[i][:].rearrange("p (e m) t -> p e m t", e=PAIR)[
-                        :, :, first // PAIR : (first + FAN_BANK) // PAIR, :
-                    ],
-                    in_=fanned[i, b][:],
-                )
-
-        def fan_block(i):
-            for b in range(FANS(i)):
-                fanned[i, b] = acc_pool.tile(
-                    [P, PAIR, P, PACK], BF16, name="fanned", tag=bank_tags[fan_count["n"] % len(bank_tags)]
-                )
-                fan_count["n"] += 1
-                first = BLOCK_COLS - (b + 1) * FAN_BANK
-                for t in range(PACK):
-                    nc.tensor.matmul(
-                        out=fanned[i, b][:, :, :, t].rearrange("p e m -> p m e"),
-                        lhsT=ident[:],
-                        rhs=raw[i][:, t, first : first + FAN_BANK].rearrange("p (m e) -> p m e", e=PAIR),
-                        start=True,
-                        stop=True,
-                    )
-
         def regroup_block(i):
-            grouped[i] = grouped_pool.tile(
-                [P, BLOCK_COLS, PACK], BF16, name="grouped", tag="grouped", align_bytes=64
-            )
+            width = block_rows(i).shape[1]
+            grouped[i] = grouped_pool.tile([P, width, PACK], BF16, name="grouped", tag="grouped", align_bytes=64)
             if blocks[i][0] == "proj":
-                for first, vec_cols, last in LAST_CUTS if i == n_blocks - 1 else ((0, VEC_COLS, BLOCK_COLS),):
+                for first, vec_cols, last in LAST_CUTS if i == n_blocks - 1 else ((0, VEC_PROJ, BLOCK_COLS),):
                     regroup(nc.vector.tensor_copy, grouped[i][:, first:vec_cols, :], raw[i][:, :, first:vec_cols])
                     regroup(nc.scalar.copy, grouped[i][:, vec_cols:last, :], raw[i][:, :, vec_cols:last])
             else:
-                n = FANS(i)
-                vec_cols = VEC(i, n)
-                last = BLOCK_COLS - n * FAN_BANK
+                vec_cols = (VEC_HEAD if i < PASSES else VEC_COLS) * width // BLOCK_COLS
                 regroup_gate(nc.vector.tensor_copy, grouped[i], raw[i], 0, vec_cols)
-                if vec_cols < last:
-                    regroup_gate(nc.scalar.copy, grouped[i], raw[i], vec_cols, last)
+                regroup_gate(nc.scalar.copy, grouped[i], raw[i], vec_cols, width)
 
         def quantise_block(i):
             kind, wide, c = blocks[i]
             if kind == "gate":
-                if c == 0:
-                    gate_codes[wide] = gate_pool.tile(
+                first, width = RANGES[wide]
+                slot, offset = divmod(first, BLOCK_COLS)
+                if c == 0 and offset == 0:
+                    gate_codes[slot] = gate_pool.tile(
                         [P, PASSES, BLOCK_COLS], U32, name="gate_codes", tag="gate_codes", align_bytes=64
                     )
-                    gate_scales[wide] = gate_pool.tile(
+                    gate_scales[slot] = gate_pool.tile(
                         [P, PASSES, BLOCK_COLS], U8, name="gate_scales", tag="gate_scales", align_bytes=64
                     )
-                codes, scales = gate_codes[wide][:, c, :], gate_scales[wide][:, c, :]
+                here = slice(offset, offset + width)
+                codes, scales = gate_codes[slot][:, c, here], gate_scales[slot][:, c, here]
             else:
                 codes, scales = proj_codes[:, c, :], proj_scales[:, c, :]
-            for cols in HALF_COLS if i == n_blocks - 1 else (slice(0, BLOCK_COLS),):
+            for cols in HALF_COLS if i == n_blocks - 1 else (slice(0, codes.shape[1]),):
                 if i == n_blocks - 1 and cols == HALF_COLS[-1]:
                     quantise_gated()
                 nc.vector.quantize_mx(
@@ -207,23 +178,37 @@ def tile_titanstnt_pb_kernel(
                     in_=grouped[i][:, cols, :].rearrange("p n t -> p (n t)"),
                 )
 
-        def gate_matmuls(e):
-            wide, piece = divmod(e, CHUNKS_PER_WIDE)
-            column_run, parity = divmod(piece, PAIR)
-            first_col = parity * (BLOCK_COLS // PAIR) + column_run * P
+        def gate_passes(e, grp, passes):
+            [(begin, width)] = [r for r in RANGES if r[0] <= e * P < r[0] + r[1]]
+            slot, offset = divmod(begin, BLOCK_COLS)
+            column_run, parity = divmod(e - begin // P, PAIR)
+            first_col = offset + parity * (width // PAIR) + column_run * P
             cols = slice(first_col, first_col + P)
+            first, count = TOKEN_GROUPS[grp]
+            for c in passes:
+                nc.tensor.matmul_mx(
+                    out=z[e][:, first : first + count],
+                    lhsT=gate_codes[slot][:, c, cols].bitcast(FP8X4),
+                    lhsT_scale=gate_scales[slot][:, c, cols],
+                    rhs=act_codes[:, c, first : first + count].bitcast(FP8X4),
+                    rhs_scale=act_scales[:, c, first : first + count],
+                    start=(c == 0),
+                    stop=(c == PASSES - 1),
+                )
+
+        def gate_matmuls(e):
             z[e] = work.tile([P, TOKENS], F32, name="z", tag="work")
-            for grp, (first, count) in enumerate(TOKEN_GROUPS):
-                for c in range(PASSES):
-                    nc.tensor.matmul_mx(
-                        out=z[e][:, first : first + count],
-                        lhsT=gate_codes[wide][:, c, cols].bitcast(FP8X4),
-                        lhsT_scale=gate_scales[wide][:, c, cols],
-                        rhs=act_codes[:, c, first : first + count].bitcast(FP8X4),
-                        rhs_scale=act_scales[:, c, first : first + count],
-                        start=(c == 0),
-                        stop=(c == PASSES - 1),
-                    )
+            for grp in range(len(TOKEN_GROUPS)):
+                gate_passes(e, grp, range(PASSES))
+
+        def gate_early(c):
+            for n, e in enumerate(EARLY):
+                if c == 0:
+                    a, h = divmod(n, HALVES)
+                    z[e] = acc_pool.tile([P, TOKENS], F32, name="z_early", tag="bank%d%d" % (a, h))
+                gate_passes(e, 0, (c,))
+                if c == PASSES - 1:
+                    gate_passes(e, 1, range(PASSES))
 
         def joined(g):
             return (g // PAIR * PAIR, PAIR) if g < PASSES - PAIR else (g, 1)
@@ -290,23 +275,20 @@ def tile_titanstnt_pb_kernel(
 
         def step(i):
             if i >= 1 and blocks[i - 1][0] == "gate" and blocks[i - 1][2] == PASSES - 1:
-                chunks["ready"] += CHUNKS_PER_WIDE
-            due = PACE(i)
-            advance = max(0, min(due, chunks["ready"]) - chunks["entered"])
+                chunks["ready"] += RANGES[blocks[i - 1][1]][1] // P
+            early = i >= 1 and blocks[i - 1][0] == "gate" and blocks[i - 1][1] == len(RANGES) - 1
+            due = PACE(sum(PAIR * block_rows(j).shape[1] // BLOCK_COLS for j in range(min(i, n_blocks))))
+            advance = max(0, min(due, chunks["ready"], EARLY[0] if chunks["entered"] <= EARLY[0] else CHUNKS) - chunks["entered"])
             advance = min(advance, MAX_ADV)
             first_left = chunks["left"]
-            chunks["left"] = max(first_left, min(chunks["entered"], chunks["entered"] + advance - Z_BANKS + EAGER))
-            if chunks["entered"] == CHUNKS:
-                chunks["left"] = CHUNKS
+            if chunks["entered"] > EARLY[-1]:
+                chunks["left"] = min(chunks["entered"], first_left + LATE_SIGMOIDS)
+            else:
+                chunks["left"] = max(first_left, min(chunks["entered"], chunks["entered"] + advance - Z_BANKS + EAGER))
             for e in range(first_left, chunks["left"]):
                 gate_sigmoid(e)
-            if FAN_LATE and i >= 1:
-                fan_copies(i - 1)
             if i < n_blocks:
-                fan_block(i)
                 regroup_block(i)
-                if not FAN_LATE:
-                    fan_copies(i)
             if i + LOOKAHEAD < n_blocks:
                 load_block(i + LOOKAHEAD)
             if i < n_blocks:
@@ -316,12 +298,18 @@ def tile_titanstnt_pb_kernel(
             for e in range(first_left, chunks["left"]):
                 if e % PACK == PACK - 1:
                     gate_product(e // PACK)
+            if early and blocks[i - 1][2] == PASSES - 1:
+                assert chunks["entered"] == EARLY[0]
+                chunks["entered"] += len(EARLY)
+                advance = 0
             for e in range(chunks["entered"], chunks["entered"] + advance):
                 gate_matmuls(e)
             chunks["entered"] += advance
+            if early:
+                gate_early(blocks[i - 1][2])
             if i >= 1 and blocks[i - 1][0] == "proj":
                 chunks["weights"] += 1
-            while chunks["projected"] < min(chunks["weights"], chunks["gated"]):
+            while chunks["left"] > EARLY[-1] and chunks["projected"] < min(chunks["weights"], chunks["gated"]):
                 project(chunks["projected"])
                 chunks["projected"] += 1
 
@@ -498,20 +486,20 @@ def tile_titanstnt_pb_kernel(
         residuals(1)
         apply_gain(0)
         finish_on_tensor(0, 0)
+        finish_on_tensor(0, 1)
         find_mean(1)
         find_deviation(1)
         empty(0, 0)
         add_bias(2, 0)
         add_bias(2, 1)
-        find_mean(2)
-        find_deviation(2)
-        finish_on_tensor(0, 1)
+        empty(0, 1)
         residuals(2)
         apply_gain(1)
         finish_on_tensor(1, 0)
-        finish_on_vector(1, 1)
-        empty(0, 1)
+        find_mean(2)
+        find_deviation(2)
         apply_gain(2)
+        finish_on_vector(1, 1)
         finish_on_vector(2, 0)
         empty(1, 0)
         finish_on_vector(2, 1)

@@ -42,9 +42,9 @@ LATE_SIGMOIDS = 3
 PROJ_EARLY = 1
 VEC_COLS = 480
 VEC_HEAD = 576
-VEC_PROJ = 416
+VEC_PROJ = 432
 HALF_COLS = (slice(0, 512), slice(512, 1024))
-LAST_CUTS = ((0, 256, 512), (512, 768, 1024))
+LAST_CUTS = ((0, 128, 512), (512, 640, 1024))
 PAIR = 2
 HALVES_OF_PASS = 2
 BY_TENSOR = ((0, 0), (0, 1), (1, 0))
@@ -120,6 +120,12 @@ def tile_titanstnt_pb_kernel(
         def load_block(i):
             width = block_rows(i).shape[1]
             raw[i] = raw_pool.tile([P, PACK, width], BF16, name="raw", tag="raw")
+            if blocks[i][0] == "proj" and i != n_blocks - 1:
+                nc.sync.dma_start(
+                    out=raw[i][:].rearrange("p (u e) n -> p u (e n)", e=PAIR),
+                    in_=block_rows(i).rearrange("(u p e) n -> p u (e n)", p=P, e=PAIR),
+                )
+                return
             for cols in HALF_COLS if i in (0, n_blocks - 1) else (slice(0, width),):
                 for u in range(HALVES_OF_PASS):
                     nc.sync.dma_start(

@@ -142,9 +142,9 @@ def tile_titanstnt_pb_kernel(
         def regroup_gate(copy, dst, src, first, last):
             copy(
                 out=dst[:].rearrange("p (e m) t -> p e m t", e=PAIR)[:, :, first // PAIR : last // PAIR, :].rearrange(
-                    "p e (c i) t -> p e c t i", i=RUN
+                    "p e (c i) t -> p c t e i", i=RUN
                 ),
-                in_=src[:, :, first:last].rearrange("p t (c i e) -> p e c t i", i=RUN, e=PAIR),
+                in_=src[:, :, first:last].rearrange("p t (c i e) -> p c t e i", i=RUN, e=PAIR),
             )
 
         def regroup_block(i):

@@ -42,7 +42,7 @@ LATE_SIGMOIDS = 3
 PROJ_EARLY = 1
 VEC_COLS = 480
 VEC_HEAD = 576
-VEC_PROJ = 432
+VEC_PROJ = 416
 HALF_COLS = (slice(0, 512), slice(512, 1024))
 LAST_CUTS = ((0, 128, 512), (512, 640, 1024))
 PAIR = 2
@@ -217,7 +217,7 @@ def tile_titanstnt_pb_kernel(
                     gate_passes(e, 1, range(PASSES))
 
         def joined(g):
-            return (g // PAIR * PAIR, PAIR) if g < PASSES - PAIR else (g, 1)
+            return (0, PASSES - PAIR) if g < PASSES - PAIR else (g, 1)
 
         def gate_sigmoid(e):
             g, t = divmod(e, PACK)
@@ -239,7 +239,7 @@ def tile_titanstnt_pb_kernel(
         def gate_product(g):
             first, count = joined(g)
             if g == first:
-                gated[first] = gating.tile([P, count, TOKENS, PACK], BF16, name="gated", tag="gated", align_bytes=64)
+                gated[first] = gating.tile([P, count, TOKENS, PACK], BF16, name="gated", tag="gated", bufs=1, align_bytes=64)
             nc.vector.tensor_tensor(
                 out=gated[first][:, g - first, :, :].rearrange("p (c i) t -> p c t i", i=RUN),
                 in0=gate[g][:].rearrange("p t (c i) -> p c t i", i=RUN),
@@ -399,6 +399,7 @@ def tile_titanstnt_pb_kernel(
         diag = {}
         residual = {}
         squares = tail.tile([P, D], BF16, name="squares")
+        scaled_sums = tail.tile([P, HALVES], F32, name="scaled_sums")
 
         def add_bias(a, h):
             if h == 0:
@@ -425,13 +426,8 @@ def tile_titanstnt_pb_kernel(
 
         def find_mean(a):
             neg_mean[a] = tail.tile([P, 1], F32, name="neg_mean%d" % a)
-            nc.vector.tensor_scalar(
-                out=neg_mean[a][:],
-                in0=sums[a][:, 0:1],
-                scalar1=sums[a][:, 1:2],
-                scalar2=-1.0 / D,
-                op0=ALU.add,
-                op1=ALU.mult,
+            nc.scalar.activation(
+                out=scaled_sums[:], in_=sums[a][:], func=ACT.Copy, scale=-1.0 / D, accum_out=neg_mean[a][:]
             )
 
         def find_deviation(a):
@@ -485,9 +481,9 @@ def tile_titanstnt_pb_kernel(
         add_bias(0, 0)
         add_bias(0, 1)
         residuals(0)
-        add_bias(1, 0)
         find_mean(0)
         find_deviation(0)
+        add_bias(1, 0)
         add_bias(1, 1)
         residuals(1)
         apply_gain(0)
@@ -498,11 +494,11 @@ def tile_titanstnt_pb_kernel(
         empty(0, 0)
         add_bias(2, 0)
         add_bias(2, 1)
+        find_mean(2)
         empty(0, 1)
         residuals(2)
         apply_gain(1)
         finish_on_tensor(1, 0)
-        find_mean(2)
         find_deviation(2)
         apply_gain(2)
         finish_on_vector(1, 1)

@@ -42,6 +42,7 @@ LATE_SIGMOIDS = 3
 PROJ_EARLY = 1
 VEC_COLS = 480
 VEC_HEAD = 576
+VEC_FIRST = 512
 VEC_PROJ = 416
 HALF_COLS = (slice(0, 512), slice(512, 1024))
 LAST_CUTS = ((0, 128, 512), (512, 640, 1024))
@@ -120,12 +121,6 @@ def tile_titanstnt_pb_kernel(
         def load_block(i):
             width = block_rows(i).shape[1]
             raw[i] = raw_pool.tile([P, PACK, width], BF16, name="raw", tag="raw")
-            if blocks[i][0] == "proj" and i != n_blocks - 1:
-                nc.sync.dma_start(
-                    out=raw[i][:].rearrange("p (u e) n -> p u (e n)", e=PAIR),
-                    in_=block_rows(i).rearrange("(u p e) n -> p u (e n)", p=P, e=PAIR),
-                )
-                return
             for cols in HALF_COLS if i in (0, n_blocks - 1) else (slice(0, width),):
                 for u in range(HALVES_OF_PASS):
                     nc.sync.dma_start(
@@ -155,7 +150,7 @@ def tile_titanstnt_pb_kernel(
                     regroup(nc.vector.tensor_copy, grouped[i][:, first:vec_cols, :], raw[i][:, :, first:vec_cols])
                     regroup(nc.scalar.copy, grouped[i][:, vec_cols:last, :], raw[i][:, :, vec_cols:last])
             else:
-                vec_cols = (VEC_HEAD if i < PASSES else VEC_COLS) * width // BLOCK_COLS
+                vec_cols = VEC_FIRST if i == 0 else VEC_HEAD if i < PASSES else VEC_COLS
                 regroup_gate(nc.vector.tensor_copy, grouped[i], raw[i], 0, vec_cols)
                 regroup_gate(nc.scalar.copy, grouped[i], raw[i], vec_cols, width)
 

@@ -134,12 +134,12 @@ def tile_titanstnt_pb_kernel(
                 in_=src.rearrange("p t (c i) -> p c t i", i=LINE),
             )
 
-        def regroup_gate(copy, dst, src, first, last):
+        def regroup_gate(copy, dst, src, first, last, order, run):
             copy(
                 out=dst[:].rearrange("p (e m) t -> p e m t", e=PAIR)[:, :, first // PAIR : last // PAIR, :].rearrange(
-                    "p e (c i) t -> p c t e i", i=RUN
+                    "p e (c i) t -> " + order, i=run
                 ),
-                in_=src[:, :, first:last].rearrange("p t (c i e) -> p c t e i", i=RUN, e=PAIR),
+                in_=src[:, :, first:last].rearrange("p t (c i e) -> " + order, i=run, e=PAIR),
             )
 
         def regroup_block(i):
@@ -151,8 +151,8 @@ def tile_titanstnt_pb_kernel(
                     regroup(nc.scalar.copy, grouped[i][:, vec_cols:last, :], raw[i][:, :, vec_cols:last])
             else:
                 vec_cols = VEC_FIRST if i == 0 else VEC_HEAD if i < PASSES else VEC_COLS
-                regroup_gate(nc.vector.tensor_copy, grouped[i], raw[i], 0, vec_cols)
-                regroup_gate(nc.scalar.copy, grouped[i], raw[i], vec_cols, width)
+                regroup_gate(nc.vector.tensor_copy, grouped[i], raw[i], 0, vec_cols, "p c t e i", RUN)
+                regroup_gate(nc.scalar.copy, grouped[i], raw[i], vec_cols, width, "p e c t i", LINE)
 
         def quantise_block(i):
             kind, wide, c = blocks[i]

from contextlib import ExitStack

import concourse.mybir as mybir
from concourse.masks import make_identity

BF16 = mybir.dt.bfloat16
F32 = mybir.dt.float32
U32 = mybir.dt.uint32
U8 = mybir.dt.uint8
FP8X4 = mybir.dt.float8_e4m3fn_x4
ALU = mybir.AluOpType
ACT = mybir.ActivationFunctionType

P = 128
PACK = 4
K_PASS = P * PACK
TOKENS = 384
TOKEN_TILES = TOKENS // P
D = 1024
WORDS = D // 2
ACT_VEC = ()
MAX_ADV = 2
EAGER = 0
PACE = lambda h: max(0, (3 * (h - 12)) // 4)
HEAD_LOADS = (("b",0),("b",1),("s",0),("b",2),("b",3),("s",1))
HEAD = (("b",0),("b",1),("load",2),("s",0),("b",2),("q",0),("b",3),("s",1),("b",4),("q",1),("b",5),("s",2),("b",6),("q",2))
STREAMS = 3
C = STREAMS * D
PASSES = C // K_PASS
PASSES_PER_STREAM = D // K_PASS
BANK = 512
HALVES = D // BANK
EPS = 1e-5

TOKEN_GROUPS = ((0, 256), (256, 128))

BLOCK_COLS = 1024
RANGES = ((0, 1024), (1024, 1024), (2048, 1024))
CHUNKS = C // P
EARLY = range(16, 22)
LATE_SIGMOIDS = 3
PROJ_EARLY = 1
VEC_COLS = 480
VEC_HEAD = 576
VEC_FIRST = 512
VEC_PROJ = 416
HALF_COLS = (slice(0, 512), slice(512, 1024))
LAST_CUTS = ((0, 128, 512), (512, 640, 1024))
PAIR = 2
HALVES_OF_PASS = 2
BY_TENSOR = ((0, 0), (0, 1), (1, 0))
LINE = 8
RUN = 4

LOOKAHEAD = 4
Z_BANKS = 2
BLOCKS_PER_STREAM = PASSES // STREAMS

FLOPS = 2 * TOKENS * C * (C + D)


def tile_titanstnt_pb_kernel(
    tc, x, global_out, local_out, core_out, gate_w, gate_b, outproj_w, outproj_b, ln_mem_g, ln_mem_b, out
):
    nc = tc.nc
    streams = [s.flatten_outer_dims() for s in (global_out, local_out, core_out)]
    x_rows = x.flatten_outer_dims()
    out_rows = out.flatten_outer_dims()

    gate_blocks = [("gate", wide, c) for wide in range(len(RANGES)) for c in range(PASSES)]
    proj_blocks = [("proj", None, g) for g in range(PASSES)]
    blocks = gate_blocks[:-PASSES] + proj_blocks[:PROJ_EARLY] + gate_blocks[-PASSES:] + proj_blocks[PROJ_EARLY:]
    n_blocks = len(blocks)

    with ExitStack() as ctx:
        ctx.enter_context(tc.manual_schedule())
        keep = ctx.enter_context(tc.tile_pool(name="keep", bufs=1))
        gate_pool = ctx.enter_context(tc.tile_pool(name="gate_pool", bufs=2))
        gating = ctx.enter_context(tc.tile_pool(name="gating", bufs=2))
        acc_pool = ctx.enter_context(tc.psum_pool(name="acc_pool", bufs=1))
        work = ctx.enter_context(tc.psum_pool(name="work", bufs=2))

        ident = keep.tile([P, P], BF16, name="ident")
        ident_words = keep.tile([P, P], F32, name="ident_words")
        gate_bias = keep.tile([P, CHUNKS], F32, name="gate_bias")
        eps = keep.tile([P, 1], F32, name="eps")
        table_in = keep.tile([P, 1], F32, name="table_in")
        table_out = keep.tile([P, 1], F32, name="table_out")
        act_grouped = keep.tile([P, PASSES, TOKENS, PACK], BF16, name="act_grouped", align_bytes=64)
        act_codes = keep.tile([P, PASSES, TOKENS], U32, name="act_codes", align_bytes=64)
        act_scales = keep.tile([P, PASSES, TOKENS], U8, name="act_scales", align_bytes=64)
        gated_codes = keep.tile([P, PASSES, TOKENS], U32, name="gated_codes", align_bytes=64)
        gated_scales = keep.tile([P, PASSES, TOKENS], U8, name="gated_scales", align_bytes=64)
        proj_codes = keep.tile([P, PASSES, D], U32, name="proj_codes", align_bytes=64)
        proj_scales = keep.tile([P, PASSES, D], U8, name="proj_scales", align_bytes=64)
        x_sb = keep.tile([P, TOKEN_TILES, D], BF16, name="x_sb")
        proj_bias = keep.tile([P, D], BF16, name="proj_bias")
        ln_gain = keep.tile([P, D], BF16, name="ln_gain")
        ones = keep.tile([P, P], BF16, name="ones")
        ln_bias_row = keep.tile([P, D], BF16, name="ln_bias_row")
        acc = {}

        raw = {}
        grouped = {}
        gate_codes = {}
        gate_scales = {}
        z = {}
        gate = {}
        gated = {}
        pending = []
        chunks = {"entered": 0, "left": 0, "weights": 0, "gated": 0, "projected": 0, "ready": 0}

        def block_rows(i):
            kind, wide, c = blocks[i]
            k_rows = slice(c * K_PASS, (c + 1) * K_PASS)
            if kind == "gate":
                first, width = RANGES[wide]
                return gate_w[k_rows, first : first + width]
            return outproj_w[k_rows, :]

        def load_block(i):
            width = block_rows(i).shape[1]
            raw[i] = raw_pool.tile([P, PACK, width], BF16, name="raw", tag="raw")
            for cols in HALF_COLS if i in (0, n_blocks - 1) else (slice(0, width),):
                for u in range(HALVES_OF_PASS):
                    nc.sync.dma_start(
                        out=raw[i][:, PAIR * u : PAIR * (u + 1), cols],
                        in_=block_rows(i)[u * 2 * P : (u + 1) * 2 * P, cols].rearrange("(p e) n -> p e n", e=PAIR),
                    )

        def regroup(copy, dst, src):
            copy(
                out=dst.rearrange("p (c i) t -> p c t i", i=LINE),
                in_=src.rearrange("p t (c i) -> p c t i", i=LINE),
            )

        def regroup_gate(copy, dst, src, first, last, order, run):
            copy(
                out=dst[:].rearrange("p (e m) t -> p e m t", e=PAIR)[:, :, first // PAIR : last // PAIR, :].rearrange(
                    "p e (c i) t -> " + order, i=run
                ),
                in_=src[:, :, first:last].rearrange("p t (c i e) -> " + order, i=run, e=PAIR),
            )

        def regroup_block(i):
            width = block_rows(i).shape[1]
            grouped[i] = grouped_pool.tile([P, width, PACK], BF16, name="grouped", tag="grouped", align_bytes=64)
            if blocks[i][0] == "proj":
                for first, vec_cols, last in LAST_CUTS if i == n_blocks - 1 else ((0, VEC_PROJ, BLOCK_COLS),):
                    regroup(nc.vector.tensor_copy, grouped[i][:, first:vec_cols, :], raw[i][:, :, first:vec_cols])
                    regroup(nc.scalar.copy, grouped[i][:, vec_cols:last, :], raw[i][:, :, vec_cols:last])
            else:
                vec_cols = VEC_FIRST if i == 0 else VEC_HEAD if i < PASSES else VEC_COLS
                regroup_gate(nc.vector.tensor_copy, grouped[i], raw[i], 0, vec_cols, "p c t e i", RUN)
                regroup_gate(nc.scalar.copy, grouped[i], raw[i], vec_cols, width, "p e c t i", LINE)

        def quantise_block(i):
            kind, wide, c = blocks[i]
            if kind == "gate":
                first, width = RANGES[wide]
                slot, offset = divmod(first, BLOCK_COLS)
                if c == 0 and offset == 0:
                    gate_codes[slot] = gate_pool.tile(
                        [P, PASSES, BLOCK_COLS], U32, name="gate_codes", tag="gate_codes", align_bytes=64
                    )
                    gate_scales[slot] = gate_pool.tile(
                        [P, PASSES, BLOCK_COLS], U8, name="gate_scales", tag="gate_scales", align_bytes=64
                    )
                here = slice(offset, offset + width)
                codes, scales = gate_codes[slot][:, c, here], gate_scales[slot][:, c, here]
            else:
                codes, scales = proj_codes[:, c, :], proj_scales[:, c, :]
            for cols in HALF_COLS if i == n_blocks - 1 else (slice(0, codes.shape[1]),):
                if i == n_blocks - 1 and cols == HALF_COLS[-1]:
                    quantise_gated()
                nc.vector.quantize_mx(
                    out=codes[:, cols].bitcast(FP8X4),
                    scales=scales[:, cols],
                    in_=grouped[i][:, cols, :].rearrange("p n t -> p (n t)"),
                )

        def gate_passes(e, grp, passes):
            [(begin, width)] = [r for r in RANGES if r[0] <= e * P < r[0] + r[1]]
            slot, offset = divmod(begin, BLOCK_COLS)
            column_run, parity = divmod(e - begin // P, PAIR)
            first_col = offset + parity * (width // PAIR) + column_run * P
            cols = slice(first_col, first_col + P)
            first, count = TOKEN_GROUPS[grp]
            for c in passes:
                nc.tensor.matmul_mx(
                    out=z[e][:, first : first + count],
                    lhsT=gate_codes[slot][:, c, cols].bitcast(FP8X4),
                    lhsT_scale=gate_scales[slot][:, c, cols],
                    rhs=act_codes[:, c, first : first + count].bitcast(FP8X4),
                    rhs_scale=act_scales[:, c, first : first + count],
                    start=(c == 0),
                    stop=(c == PASSES - 1),
                )

        def gate_matmuls(e):
            z[e] = work.tile([P, TOKENS], F32, name="z", tag="work")
            for grp in range(len(TOKEN_GROUPS)):
                gate_passes(e, grp, range(PASSES))

        def gate_early(c):
            for n, e in enumerate(EARLY):
                if c == 0:
                    a, h = divmod(n, HALVES)
                    z[e] = acc_pool.tile([P, TOKENS], F32, name="z_early", tag="bank%d%d" % (a, h))
                gate_passes(e, 0, (c,))
                if c == PASSES - 1:
                    gate_passes(e, 1, range(PASSES))

        def joined(g):
            return (0, PASSES - PAIR) if g < PASSES - PAIR else (g, 1)

        def gate_sigmoid(e):
            g, t = divmod(e, PACK)
            if t == 0:
                gate[g] = gating.tile([P, PACK, TOKENS], F32, name="gate", tag="gate")
            nc.scalar.activation(
                out=gate[g][:, t, :], in_=z[e][:], func=ACT.Sigmoid, bias=gate_bias[:, e : e + 1], scale=1.0
            )

        def quantise_runs(codes, scales, values):
            words = codes.shape[1]
            for run in (slice(0, 2 * words // 3), slice(2 * words // 3, words)):
                nc.vector.quantize_mx(
                    out=codes[:, run].bitcast(FP8X4),
                    scales=scales[:, run],
                    in_=values[:, run, :].rearrange("p w t -> p (w t)"),
                )

        def gate_product(g):
            first, count = joined(g)
            if g == first:
                gated[first] = gating.tile([P, count, TOKENS, PACK], BF16, name="gated", tag="gated", bufs=1, align_bytes=64)
            nc.vector.tensor_tensor(
                out=gated[first][:, g - first, :, :].rearrange("p (c i) t -> p c t i", i=RUN),
                in0=gate[g][:].rearrange("p t (c i) -> p c t i", i=RUN),
                in1=act_grouped[:, g, :, :].rearrange("p (c i) t -> p c t i", i=RUN),
                op=ALU.mult,
            )
            if g == first + count - 1:
                pending.append(first)

        def quantise_gated():
            while pending:
                first, count = joined(pending.pop(0))
                span = slice(first, first + count)
                quantise_runs(
                    gated_codes[:, span, :].rearrange("p c k -> p (c k)"),
                    gated_scales[:, span, :].rearrange("p c k -> p (c k)"),
                    gated[first][:].rearrange("p c k t -> p (c k) t"),
                )
                chunks["gated"] += count

        def project(g):
            pairs = [(a, h) for a in range(TOKEN_TILES) for h in range(HALVES)]
            if g == PASSES - 1:
                pairs = sorted(pairs, key=lambda pair: pair[1])
            for a, h in pairs:
                if g == 0:
                    acc[a, h] = acc_pool.tile([P, BANK], F32, name="acc%d%d" % (a, h), tag="bank%d%d" % (a, h))
                toks = slice(a * P, (a + 1) * P)
                cols = slice(h * BANK, (h + 1) * BANK)
                nc.tensor.matmul_mx(
                    out=acc[a, h][:],
                    lhsT=gated_codes[:, g, toks].bitcast(FP8X4),
                    lhsT_scale=gated_scales[:, g, toks],
                    rhs=proj_codes[:, g, cols].bitcast(FP8X4),
                    rhs_scale=proj_scales[:, g, cols],
                    start=(g == 0),
                    stop=(g == PASSES - 1),
                )

        def step(i):
            if i >= 1 and blocks[i - 1][0] == "gate" and blocks[i - 1][2] == PASSES - 1:
                chunks["ready"] += RANGES[blocks[i - 1][1]][1] // P
            early = i >= 1 and blocks[i - 1][0] == "gate" and blocks[i - 1][1] == len(RANGES) - 1
            due = PACE(sum(PAIR * block_rows(j).shape[1] // BLOCK_COLS for j in range(min(i, n_blocks))))
            advance = max(0, min(due, chunks["ready"], EARLY[0] if chunks["entered"] <= EARLY[0] else CHUNKS) - chunks["entered"])
            advance = min(advance, MAX_ADV)
            first_left = chunks["left"]
            if chunks["entered"] > EARLY[-1]:
                chunks["left"] = min(chunks["entered"], first_left + LATE_SIGMOIDS)
            else:
                chunks["left"] = max(first_left, min(chunks["entered"], chunks["entered"] + advance - Z_BANKS + EAGER))
            for e in range(first_left, chunks["left"]):
                gate_sigmoid(e)
            if i < n_blocks:
                regroup_block(i)
            if i + LOOKAHEAD < n_blocks:
                load_block(i + LOOKAHEAD)
            if i < n_blocks:
                quantise_gated()
            if i >= 1:
                quantise_block(i - 1)
            for e in range(first_left, chunks["left"]):
                if e % PACK == PACK - 1:
                    gate_product(e // PACK)
            if early and blocks[i - 1][2] == PASSES - 1:
                assert chunks["entered"] == EARLY[0]
                chunks["entered"] += len(EARLY)
                advance = 0
            for e in range(chunks["entered"], chunks["entered"] + advance):
                gate_matmuls(e)
            chunks["entered"] += advance
            if early:
                gate_early(blocks[i - 1][2])
            if i >= 1 and blocks[i - 1][0] == "proj":
                chunks["weights"] += 1
            while chunks["left"] > EARLY[-1] and chunks["projected"] < min(chunks["weights"], chunks["gated"]):
                project(chunks["projected"])
                chunks["projected"] += 1

        with ExitStack() as stage:
            raw_pool = stage.enter_context(tc.tile_pool(name="raw_pool", bufs=LOOKAHEAD))
            grouped_pool = stage.enter_context(tc.tile_pool(name="grouped_pool", bufs=3))
            acts = stage.enter_context(tc.tile_pool(name="acts", bufs=1))

            nc.vector.memset(table_in[:], 0.0)
            nc.scalar.activation(out=table_out[:], in_=table_in[:], func=ACT.Sigmoid)
            act_rows = {}

            def load_stream(s):
                for a in range(TOKEN_TILES):
                    act_rows[s, a] = acts.tile([P, D], BF16, name="act_rows", tag="act_rows%d" % a, bufs=2)
                    nc.sync.dma_start(out=act_rows[s, a][:], in_=streams[s][a * P : (a + 1) * P, :])

            for what, which in HEAD_LOADS:
                (load_block if what == "b" else load_stream)(which)

            make_identity(nc, ident_words[:])
            nc.vector.tensor_copy(out=ident[:], in_=ident_words[:])
            nc.vector.memset(eps[:], EPS)
            nc.vector.memset(ones[:], 1.0)
            nc.vector.memset(ln_bias_row[:], 0.0)

            def quantise_stream(s):
                passes = slice(s * PASSES_PER_STREAM, (s + 1) * PASSES_PER_STREAM)
                quantise_runs(
                    act_codes[:, passes, :].rearrange("p c k -> p (c k)"),
                    act_scales[:, passes, :].rearrange("p c k -> p (c k)"),
                    act_grouped[:, passes, :, :].rearrange("p c k t -> p (c k) t"),
                )

            def do_stream(s):
                passes = slice(s * PASSES_PER_STREAM, (s + 1) * PASSES_PER_STREAM)
                for a in range(TOKEN_TILES):
                    turned = work.tile([P, WORDS // P, P], F32, name="turned", tag="work")
                    for j in range(WORDS // P):
                        nc.tensor.transpose(
                            turned[:, j, :], act_rows[s, a][:].bitcast(F32)[:, j * P : (j + 1) * P], ident_words[:]
                        )
                    toks = slice(a * P, (a + 1) * P)
                    copy = nc.vector.tensor_copy if a in ACT_VEC else nc.scalar.copy
                    copy(
                        out=act_grouped[:, passes, toks, :].bitcast(F32),
                        in_=turned[:].rearrange("p (c u) k -> p c k u", u=HALVES_OF_PASS),
                    )

            for what, which in HEAD:
                if what == "load":
                    load_stream(which)
                    bias_rows = acts.tile([P, PAIR * P], BF16, name="bias_rows")
                    nc.vector.memset(bias_rows[:], 0.0)
                    nc.sync.dma_start(out=bias_rows[: CHUNKS // PAIR, :], in_=gate_b.rearrange("(r p) -> r p", p=PAIR * P))
                else:
                    {"b": step, "s": do_stream, "q": quantise_stream}[what](which)
            first_step = 1 + max(w for what, w in HEAD if what == "b")
            bias_cols = work.tile([P, P], F32, name="bias_cols", tag="work")
            nc.tensor.transpose(bias_cols[:], bias_rows[:].bitcast(F32), ident_words[:])
            nc.vector.tensor_copy(out=gate_bias[:], in_=bias_cols[:].bitcast(BF16)[:, :CHUNKS])

            for i in range(first_step, n_blocks + 1):
                step(i)
                if i + LOOKAHEAD == n_blocks:
                    nc.sync.dma_start(out=x_sb[:], in_=x_rows.rearrange("(a p) d -> p a d", p=P))
                    nc.sync.dma_start(out=ln_bias_row[:1, :], in_=ln_mem_b.unsqueeze(0))
                    nc.sync.dma_start(out=proj_bias[:], in_=outproj_b.partition_broadcast(P))
                    nc.sync.dma_start(out=ln_gain[:], in_=ln_mem_g.partition_broadcast(P))

        assert chunks["left"] == CHUNKS and chunks["projected"] == PASSES, chunks
        tail = ctx.enter_context(tc.tile_pool(name="tail", bufs=1))

        nc.scalar.activation(out=table_out[:], in_=eps[:], func=ACT.Abs_reciprocal_sqrt)

        m = {}
        scaled = {}
        sums = {}
        neg_mean = {}
        rstd = {}
        diag = {}
        residual = {}
        squares = tail.tile([P, D], BF16, name="squares")
        scaled_sums = tail.tile([P, HALVES], F32, name="scaled_sums")

        def add_bias(a, h):
            if h == 0:
                m[a] = tail.tile([P, D], F32, name="m%d" % a)
                sums[a] = tail.tile([P, HALVES], F32, name="sums%d" % a)
            cols = slice(h * BANK, (h + 1) * BANK)
            nc.vector.scalar_tensor_tensor(
                out=m[a][:, cols],
                in0=acc[a, h][:],
                scalar=1.0,
                in1=proj_bias[:, cols],
                op0=ALU.mult,
                op1=ALU.add,
                accum_out=sums[a][:, h : h + 1],
            )

        def open_residual(a, h):
            cols = slice(h * BANK, (h + 1) * BANK)
            residual[a, h] = acc_pool.tile([P, BANK], F32, name="residual%d%d" % (a, h), tag="bank%d%d" % (a, h))
            nc.tensor.matmul(out=residual[a, h][:], lhsT=ident[:], rhs=x_sb[:, a, cols], start=True, stop=False)
            nc.tensor.matmul(
                out=residual[a, h][:], lhsT=ones[:], rhs=ln_bias_row[:, cols], start=False, stop=(a, h) not in BY_TENSOR
            )

        def find_mean(a):
            neg_mean[a] = tail.tile([P, 1], F32, name="neg_mean%d" % a)
            nc.scalar.activation(
                out=scaled_sums[:], in_=sums[a][:], func=ACT.Copy, scale=-1.0 / D, accum_out=neg_mean[a][:]
            )

        def find_deviation(a):
            sum_sq = tail.tile([P, 1], F32, name="sum_sq%d" % a)
            nc.scalar.activation(
                out=squares[:], in_=m[a][:], func=ACT.Square, bias=neg_mean[a][:], scale=1.0, accum_out=sum_sq[:]
            )
            rstd[a] = tail.tile([P, 1], F32, name="rstd%d" % a)
            nc.scalar.activation(
                out=rstd[a][:], in_=sum_sq[:], func=ACT.Abs_reciprocal_sqrt, bias=eps[:], scale=1.0 / D
            )
            if (a, 0) in BY_TENSOR:
                diag[a] = tail.tile([P, P], F32, name="diag%d" % a)
                nc.scalar.activation(out=diag[a][:], in_=ident_words[:], func=ACT.Copy, scale=rstd[a][:])

        def apply_gain(a):
            scaled[a] = tail.tile([P, D], F32, name="scaled%d" % a)
            nc.vector.scalar_tensor_tensor(
                out=scaled[a][:], in0=m[a][:], scalar=neg_mean[a][:], in1=ln_gain[:], op0=ALU.add, op1=ALU.mult
            )

        def store(a, h):
            cols = slice(h * BANK, (h + 1) * BANK)
            nc.sync.dma_start(out=out_rows[a * P : (a + 1) * P, cols], in_=m[a][:, cols])

        def finish_on_vector(a, h):
            cols = slice(h * BANK, (h + 1) * BANK)
            nc.vector.scalar_tensor_tensor(
                out=m[a][:, cols],
                in0=scaled[a][:, cols],
                scalar=rstd[a][:],
                in1=residual[a, h][:],
                op0=ALU.mult,
                op1=ALU.add,
            )
            store(a, h)

        def finish_on_tensor(a, h):
            cols = slice(h * BANK, (h + 1) * BANK)
            nc.tensor.matmul(out=residual[a, h][:], lhsT=diag[a][:], rhs=scaled[a][:, cols], start=False, stop=True)

        def empty(a, h):
            cols = slice(h * BANK, (h + 1) * BANK)
            nc.scalar.copy(out=m[a][:, cols], in_=residual[a, h][:])
            store(a, h)

        def residuals(a):
            for h in range(HALVES):
                open_residual(a, h)

        add_bias(0, 0)
        add_bias(0, 1)
        residuals(0)
        find_mean(0)
        find_deviation(0)
        add_bias(1, 0)
        add_bias(1, 1)
        residuals(1)
        apply_gain(0)
        finish_on_tensor(0, 0)
        finish_on_tensor(0, 1)
        find_mean(1)
        find_deviation(1)
        empty(0, 0)
        add_bias(2, 0)
        add_bias(2, 1)
        find_mean(2)
        empty(0, 1)
        residuals(2)
        apply_gain(1)
        finish_on_tensor(1, 0)
        find_deviation(2)
        apply_gain(2)
        finish_on_vector(1, 1)
        finish_on_vector(2, 0)
        empty(1, 0)
        finish_on_vector(2, 1)
